import numpy as np
import ml_dtypes


def mxq(x, axis, fmt="e4m3"):
    dtype, down = {"e4m3": (ml_dtypes.float8_e4m3fn, 7), "e5m2": (ml_dtypes.float8_e5m2, 14)}[fmt]
    v = np.moveaxis(np.asarray(x, np.float32).astype(ml_dtypes.bfloat16).astype(np.float64), axis, -1)
    blocks = v.reshape(v.shape[:-1] + (-1, 32))
    amax = np.abs(blocks).max(-1, keepdims=True)
    byte = np.maximum(np.where(amax > 0, np.frexp(amax)[1] - 1 + 127, 0) - down, 1)
    scale = np.exp2(byte - 127.0)
    codes = (blocks / scale).astype(np.float32).astype(dtype).astype(np.float64)
    return np.moveaxis((codes * scale).reshape(v.shape), -1, axis)


WIDE = False


def mx_kscale(k):
    if not WIDE:
        return np.ones(k)
    levels = np.array([10, -10, 5, -5, 0])
    a = np.random.permutation(np.resize(levels, k // 512 * 4)).reshape(k // 512, 4)
    idx = np.arange(k)
    return np.exp2(a[idx // 512, idx % 128 // 32])


BF16 = ml_dtypes.bfloat16


def bf(x):
    return np.asarray(x, np.float32).astype(BF16)


def f64(x):
    return np.asarray(x).astype(np.float64)


B, T, N, C = 2, 2, 512, 1024
EDGE = 0.0625


def setup_inputs():
    s = mx_kscale(C)
    return {"x": bf(np.random.standard_normal((B, T, N, C)) * 0.5 * s),
            "adj": bf(np.random.random((B, N, N)) * (np.random.random((B, N, N)) < EDGE)),
            "lam_raw": bf(3.5 + 0.1 * np.random.standard_normal(1)),
            "theta": bf(np.random.standard_normal((C, C)) * 7.5 / np.sqrt(C) / s[:, None])}


def reference(x, adj, lam_raw, theta):
    lam = 1.0 + np.maximum(f64(lam_raw)[0], 0.0)
    h = mxq(f64(x), 3, "e4m3") @ mxq(f64(theta), 0, "e4m3")
    v = ((2.0 * lam - 2.0) / lam) * np.eye(N) + (2.0 / lam) * f64(adj)
    v = v / np.sum(v, axis=-1, keepdims=True)
    out = mxq(v, 2, "e4m3")[:, None] @ mxq(h, 2, "e4m3")
    return np.maximum(out, 0.0)

@@ -1,0 +1,327 @@
+from contextlib import ExitStack
+
+import concourse.mybir as mybir
+from concourse.masks import make_identity
+
+F32 = mybir.dt.float32
+BF16 = mybir.dt.bfloat16
+U32 = mybir.dt.uint32
+U8 = mybir.dt.uint8
+FP8X4 = mybir.dt.float8_e4m3fn_x4
+ALU = mybir.AluOpType
+ACT = mybir.ActivationFunctionType
+
+P = 128
+B, T, N, C = 2, 2, 512, 1024
+FLOPS = 2 * B * T * N * C * C + 2 * B * T * N * N * C
+
+LOADS = ["a0", "t0", "x0", "t1", "x1", "a1", "x2", "x3"]
+LAG = 2
+PS_BUFS = (2, 3, 3)
+
+
+def v_steps(b, kinds, engine):
+    return [("VP", b, k, i, engine) for k in kinds for i in range(4)]
+
+
+def body(fill, hp_over, tp_over, tpos):
+    s = []
+    for u in range(8 + LAG):
+        bt, h = u // 2, u % 2
+        w = u - LAG
+        hp = hp_over.get(u, "svss")
+        op = "vsvs"
+        tpe = tp_over.get(u, "sv")
+        more_x = u < 8 and bt + 1 < B * T
+        bunch = [("T", bt + 1, h, 0, tpe[0]), ("T", bt + 1, h, 1, tpe[1])] if more_x else []
+        tp = tpos.get(u, -1)
+        qx = -2
+        s += fill.get((u, -1), [])
+        if tp == -1:
+            s += bunch
+            qx = 0
+        for k in range(4):
+            if u < 8:
+                s += [("S1", bt, h, k, hp[k])]
+            if w >= 0:
+                s += [("S2", w // 2, w % 2, k, op[k])]
+            if qx == k and more_x:
+                s += [("QX", bt + 1, h)]
+            if tp == k:
+                s += bunch
+                qx = k + 1
+            s += fill.get((u, k), [])
+        if qx == 4 and more_x:
+            s += [("QX", bt + 1, h)]
+        if u < 8:
+            s += [("QH", bt, h)]
+    return s
+
+
+def plan():
+    head = [("VP", 0, "diag", 0, "g")] + v_steps(0, ["sum"], "v") + [("VP", 0, "inv", 0, "v")]
+    head += [("THR", 0, 0, "v"), ("THR", 0, 1, "s"), ("THR", 1, 0, "v"), ("THR", 1, 1, "s"), ("THQ", 0)]
+    head += [("VP", 0, "scale", 0, "v"), ("VP", 0, "scale", 1, "v"), ("THQ", 1)]
+    head += [("VP", 0, "scale", 2, "v"), ("VP", 0, "scale", 3, "v")] + v_steps(0, ["fix"], "v")
+    head += [("T", 0, 0, 0, "s"), ("T", 0, 0, 1, "s"), ("QX", 0, 0), ("T", 0, 1, 0, "s"), ("T", 0, 1, 1, "s")]
+    head += [("THR", 2, 0, "v"), ("QX", 0, 1), ("THR", 2, 1, "v"), ("THQ", 2)]
+    second = [("VP", 1, "diag", 0, "g")] + [("VP", 1, "tree", i, "g") for i in range(4)]
+    second += [("VP", 1, "treesum", 3, "v"), ("VP", 1, "inv", 0, "v")] + v_steps(1, ["scale", "fix"], "g")
+    fill = {
+        (0, 0): [("THR", 3, 0, "v")],
+        (0, 1): [("THR", 3, 1, "v"), ("THQ", 3)],
+        (1, -1): [("VT", 0, 0, "s")],
+        (1, 2): [("VT", 0, 1, "s")],
+        (1, 3): [("QV", 0)],
+        (2, 0): second,
+        (4, -1): [("VT", 1, 0, "s")],
+        (4, 1): [("VT", 1, 1, "v")],
+        (4, 3): [("QV", 1)],
+    }
+    return head + body(fill, {0: "sssv", 1: "ssss"}, {0: "ss", 1: "vs"}, {0: 3, 1: 1})
+
+
+def tile_akgcn_pa_kernel(tc, x, adj, lam_raw, theta, out):
+    nc = tc.nc
+    with ExitStack() as ctx:
+        keep = ctx.enter_context(tc.tile_pool(name="keep", bufs=1))
+        work = ctx.enter_context(tc.tile_pool(name="work", bufs=2))
+        stage = ctx.enter_context(tc.tile_pool(name="stage", bufs=6))
+        ps_t = ctx.enter_context(tc.psum_pool(name="ps_t", bufs=PS_BUFS[0]))
+        ps_h = ctx.enter_context(tc.psum_pool(name="ps_h", bufs=PS_BUFS[1]))
+        ps_o = ctx.enter_context(tc.psum_pool(name="ps_o", bufs=PS_BUFS[2]))
+        ctx.enter_context(tc.manual_schedule())
+
+        def copy_out(engine, dst, src):
+            if engine == "s":
+                nc.scalar.copy(out=dst, in_=src)
+            else:
+                nc.vector.tensor_copy(out=dst, in_=src)
+
+        def times_column(engine, dst, src, column):
+            if engine == "s":
+                nc.scalar.activation(out=dst, in_=src, func=ACT.Copy, scale=column)
+            elif engine == "g":
+                nc.gpsimd.tensor_scalar(out=dst, in0=src, scalar1=column, scalar2=0.0, op0=ALU.mult, op1=ALU.add)
+            else:
+                nc.vector.tensor_scalar(out=dst, in0=src, scalar1=column, scalar2=None, op0=ALU.mult)
+
+        lam_sb = keep.tile([P, 1], BF16, name="lam_sb")
+        nc.scalar.dma_start(out=lam_sb[:], in_=lam_raw.partition_broadcast(P))
+        adj_sb = [keep.tile([P, 5 * N], BF16, name="adj%d" % b) for b in range(B)]
+        x_sb = [keep.tile([P, 4, C], BF16, name="x%d" % bt) for bt in range(B * T)]
+        th_raw = [keep.tile([P, 8, 512], BF16, name="th%d" % h) for h in range(2)]
+        for item in LOADS:
+            k = int(item[1])
+            if item[0] == "a":
+                nc.sync.dma_start(
+                    out=adj_sb[k][:, 0 : 4 * N].rearrange("p (i m) -> p i m", i=4),
+                    in_=adj[k].rearrange("(i p) m -> p i m", p=P),
+                )
+            elif item[0] == "x":
+                nc.sync.dma_start(out=x_sb[k][:], in_=x[k // T, k % T].rearrange("(j p) c -> p j c", p=P))
+            else:
+                src = theta.rearrange("(t q e) c -> q t e c", t=4, q=P, e=2)
+                dst = th_raw[k][:].rearrange("q (t e) c -> q t e c", e=2)
+                for e in range(2):
+                    nc.sync.dma_start(out=dst[:, :, e, :], in_=src[:, :, e, 512 * k : 512 * k + 512])
+
+        ident_f = keep.tile([P, P], F32, name="ident_f")
+        make_identity(nc, ident_f[:])
+        ident_b = keep.tile([P, P], BF16, name="ident_b")
+        make_identity(nc, ident_b[:])
+        r = keep.tile([P, 1], F32, name="r")
+        nc.vector.tensor_scalar_max(out=r[:], in0=lam_sb[:], scalar1=0.0)
+        r_eye = keep.tile([P, P], F32, name="r_eye")
+        nc.vector.tensor_scalar(out=r_eye[:], in0=ident_f[:], scalar1=r[:, 0:1], scalar2=None, op0=ALU.mult)
+
+        thc = keep.tile([P, 4, 2, 256], U32, name="thc", align_bytes=64)
+        ths = keep.tile([P, 4, 2, 256], U8, name="ths", align_bytes=64)
+        vc = [keep.tile([P, N], U32, name="vc%d" % b, align_bytes=64) for b in range(B)]
+        vs = [keep.tile([P, N], U8, name="vs%d" % b, align_bytes=64) for b in range(B)]
+        vg = [keep.tile([P, N, 4], BF16, name="vg%d" % b, align_bytes=64) for b in range(B)]
+        rowsum = [keep.tile([P, 4], F32, name="rowsum%d" % b) for b in range(B)]
+        den = [keep.tile([P, 4], F32, name="den%d" % b) for b in range(B)]
+        rinv = [keep.tile([P, 4], F32, name="rinv%d" % b) for b in range(B)]
+        wdiag = [keep.tile([P, 4, P], F32, name="wdiag%d" % b) for b in range(B)]
+        vb = [keep.tile([P, 4, N], BF16, name="vb%d" % b) for b in range(B)]
+        xq = {}
+        hq = {}
+        tgs = {}
+        tree = {}
+
+        def v_piece(b, kind, i, engine):
+            rows = adj_sb[b][:, 0 : 4 * N].rearrange("p (i m) -> p i m", i=4)
+            if kind == "diag":
+                nc.gpsimd.tensor_tensor(
+                    out=wdiag[b][:],
+                    in0=adj_sb[b][:].rearrange("p (i s) -> p i s", s=N + P)[:, :, 0:P],
+                    in1=r_eye[:].unsqueeze(1).to_broadcast([P, 4, P]),
+                    op=ALU.add,
+                )
+            elif kind == "sum":
+                if engine == "s":
+                    junk = work.tile([P, N], BF16, name="junk")
+                    nc.scalar.activation(
+                        out=junk[:], in_=rows[:, i, :], func=ACT.Copy, accum_out=rowsum[b][:, i : i + 1]
+                    )
+                else:
+                    nc.vector.tensor_reduce(
+                        out=rowsum[b][:, i : i + 1], in_=rows[:, i, :], axis=mybir.AxisListType.X, op=ALU.add
+                    )
+            elif kind == "tree":
+                width = 256 >> i
+                src = rows if i == 0 else tree[(b, i - 1)][:]
+                tree[(b, i)] = keep.tile([P, 4, width], F32, name="tree%d_%d" % (b, i))
+                nc.gpsimd.tensor_tensor(
+                    out=tree[(b, i)][:], in0=src[:, :, 0:width], in1=src[:, :, width : 2 * width], op=ALU.add
+                )
+            elif kind == "treesum":
+                nc.vector.tensor_reduce(out=rowsum[b][:], in_=tree[(b, i)][:], axis=mybir.AxisListType.X, op=ALU.add)
+            elif kind == "inv":
+                nc.vector.tensor_scalar(
+                    out=den[b][:], in0=rowsum[b][:], scalar1=r[:, 0:1], scalar2=None, op0=ALU.add
+                )
+                nc.vector.reciprocal(out=rinv[b][:], in_=den[b][:])
+            elif kind == "scale":
+                times_column(engine, vb[b][:, i, :], rows[:, i, :], rinv[b][:, i : i + 1])
+            else:
+                times_column(engine, vb[b][:, i, P * i : P * i + P], wdiag[b][:, i, :], rinv[b][:, i : i + 1])
+
+        def v_transpose(b, ip, engine):
+            vt = ps_t.tile([P, 2, 4, P], BF16, name="vt", tag="tp")
+            for i2 in range(2):
+                for j in range(4):
+                    nc.tensor.transpose(
+                        out=vt[:, i2, j, :], in_=vb[b][:, 2 * ip + i2, P * j : P * j + P], identity=ident_b[:]
+                    )
+            copy_out(
+                engine,
+                vg[b][:, 256 * ip : 256 * ip + 256, :].rearrange("p (i n) j -> p i n j", i=2),
+                vt[:].rearrange("p i j n -> p i n j"),
+            )
+
+        def x_transpose(bt, g, jp, engine):
+            if bt not in xq:
+                gx = work.tile([P, 2, N, 4], BF16, name="gx", align_bytes=64)
+                xc = work.tile([P, 2, N], U32, name="xc", align_bytes=64)
+                xs = work.tile([P, 2, N], U8, name="xs", align_bytes=64)
+                xq[bt] = (gx, xc, xs)
+            xw = x_sb[bt][:].bitcast(F32)
+            gxw = xq[bt][0][:].bitcast(F32)
+            xt = ps_t.tile([P, 2, 256], F32, name="xt", tag="tp")
+            for jj in range(2):
+                for u in range(2):
+                    lo = 256 * g + P * u
+                    nc.tensor.transpose(
+                        out=xt[:, u, P * jj : P * jj + P], in_=xw[:, 2 * jp + jj, lo : lo + P], identity=ident_f[:]
+                    )
+            copy_out(engine, gxw[:, g, 256 * jp : 256 * jp + 256, :], xt[:].rearrange("q u m -> q m u"))
+
+        def x_quantise(bt, g):
+            gx, xc, xs = xq[bt]
+            nc.vector.quantize_mx(
+                out=xc[:, g, :].bitcast(FP8X4), scales=xs[:, g, :], in_=gx[:, g].rearrange("q m t -> q (m t)")
+            )
+
+        def theta_regroup(piece, g, engine):
+            if piece not in tgs:
+                tgs[piece] = keep.tile([P, 2, 256, 4], BF16, name="tg%d" % piece, align_bytes=64)
+            lo = 256 * (piece % 2)
+            dst = tgs[piece][:, g].rearrange("p (c i) t -> p c t i", i=4)
+            src = th_raw[piece // 2][:, 4 * g : 4 * g + 4, lo : lo + 256].rearrange("p t (c i) -> p c t i", i=4)
+            if engine == "g":
+                nc.gpsimd.tensor_scalar(out=dst, in0=src, scalar1=1.0, scalar2=0.0, op0=ALU.mult, op1=ALU.add)
+            else:
+                copy_out(engine, dst, src)
+
+        def theta_quantise(piece):
+            tg = tgs[piece]
+            nc.vector.quantize_mx(
+                out=thc[:, piece].rearrange("p g c -> p (g c)").bitcast(FP8X4),
+                scales=ths[:, piece].rearrange("p g c -> p (g c)"),
+                in_=tg[:].rearrange("p g c t -> p (g c t)"),
+            )
+
+        def first_product(bt, h, c4, engine):
+            if bt not in hq:
+                hg = work.tile([P, C, 4], BF16, name="hg", align_bytes=64)
+                hc = work.tile([P, C], U32, name="hc", align_bytes=64, bufs=3)
+                hs = work.tile([P, C], U8, name="hs", align_bytes=64, bufs=3)
+                hq[bt] = (hg, hc, hs)
+            xc, xs = xq[bt][1], xq[bt][2]
+            hp = ps_h.tile([P, 4, P], F32, name="hp")
+            piece = 2 * h + c4 // 2
+            cols = slice(P * (c4 % 2), P * (c4 % 2) + P)
+            for j in range(4):
+                rows = slice(P * j, P * j + P)
+                for g in range(2):
+                    nc.tensor.matmul_mx(
+                        out=hp[:, j, :],
+                        lhsT=xc[:, g, rows].bitcast(FP8X4),
+                        lhsT_scale=xs[:, g, rows],
+                        rhs=thc[:, piece, g, cols].bitcast(FP8X4),
+                        rhs_scale=ths[:, piece, g, cols],
+                        start=(g == 0),
+                        stop=(g == 1),
+                    )
+            lo = 512 * h + P * c4
+            copy_out(engine, hq[bt][0][:, lo : lo + P, :], hp[:].rearrange("p j c -> p c j"))
+
+        def h_quantise(bt, h):
+            hg, hc, hs = hq[bt]
+            half = slice(512 * h, 512 * h + 512)
+            nc.vector.quantize_mx(
+                out=hc[:, half].bitcast(FP8X4), scales=hs[:, half], in_=hg[:, half, :].rearrange("p c j -> p (c j)")
+            )
+
+        def second_product(bt, ch, i, engine):
+            b = bt // T
+            hc, hs = hq[bt][1], hq[bt][2]
+            half = slice(512 * ch, 512 * ch + 512)
+            rows = slice(P * i, P * i + P)
+            op = ps_o.tile([P, 512], F32, name="op")
+            nc.tensor.matmul_mx(
+                out=op[:],
+                lhsT=vc[b][:, rows].bitcast(FP8X4),
+                lhsT_scale=vs[b][:, rows],
+                rhs=hc[:, half].bitcast(FP8X4),
+                rhs_scale=hs[:, half],
+                start=True,
+                stop=True,
+            )
+            ob = stage.tile([P, 512], F32, name="ob")
+            if engine == "s":
+                nc.scalar.activation(out=ob[:], in_=op[:], func=ACT.Relu)
+            else:
+                nc.vector.tensor_scalar_max(out=ob[:], in0=op[:], scalar1=0.0)
+            nc.sync.dma_start(out=out[b, bt % T, rows, half], in_=ob[:])
+
+        for tok in plan():
+            kind = tok[0]
+            if kind == "VP":
+                v_piece(tok[1], tok[2], tok[3], tok[4])
+            elif kind == "TH":
+                theta_regroup(tok[1], 0, tok[2][0])
+                theta_regroup(tok[1], 1, tok[2][1])
+                theta_quantise(tok[1])
+            elif kind == "THR":
+                theta_regroup(tok[1], tok[2], tok[3])
+            elif kind == "THQ":
+                theta_quantise(tok[1])
+            elif kind == "T":
+                x_transpose(tok[1], tok[2], tok[3], tok[4])
+            elif kind == "QX":
+                x_quantise(tok[1], tok[2])
+            elif kind == "VT":
+                v_transpose(tok[1], tok[2], tok[3])
+            elif kind == "QV":
+                nc.vector.quantize_mx(
+                    out=vc[tok[1]][:].bitcast(FP8X4), scales=vs[tok[1]][:], in_=vg[tok[1]][:].rearrange("p n j -> p (n j)")
+                )
+            elif kind == "S1":
+                first_product(tok[1], tok[2], tok[3], tok[4])
+            elif kind == "QH":
+                h_quantise(tok[1], tok[2])
+            else:
+                second_product(tok[1], tok[2], tok[3], tok[4])

@@ -15,70 +15,17 @@ P = 128
 B, T, N, C = 2, 2, 512, 1024
 FLOPS = 2 * B * T * N * C * C + 2 * B * T * N * N * C
 
-LOADS = ["a0", "t0", "x0", "t1", "x1", "a1", "x2", "x3"]
+HALF = 512
+UNITS = 2 * B * T
 LAG = 2
-PS_BUFS = (2, 3, 3)
-
-
-def v_steps(b, kinds, engine):
-    return [("VP", b, k, i, engine) for k in kinds for i in range(4)]
-
-
-def body(fill, hp_over, tp_over, tpos):
-    s = []
-    for u in range(8 + LAG):
-        bt, h = u // 2, u % 2
-        w = u - LAG
-        hp = hp_over.get(u, "svss")
-        op = "vsvs"
-        tpe = tp_over.get(u, "sv")
-        more_x = u < 8 and bt + 1 < B * T
-        bunch = [("T", bt + 1, h, 0, tpe[0]), ("T", bt + 1, h, 1, tpe[1])] if more_x else []
-        tp = tpos.get(u, -1)
-        qx = -2
-        s += fill.get((u, -1), [])
-        if tp == -1:
-            s += bunch
-            qx = 0
-        for k in range(4):
-            if u < 8:
-                s += [("S1", bt, h, k, hp[k])]
-            if w >= 0:
-                s += [("S2", w // 2, w % 2, k, op[k])]
-            if qx == k and more_x:
-                s += [("QX", bt + 1, h)]
-            if tp == k:
-                s += bunch
-                qx = k + 1
-            s += fill.get((u, k), [])
-        if qx == 4 and more_x:
-            s += [("QX", bt + 1, h)]
-        if u < 8:
-            s += [("QH", bt, h)]
-    return s
-
-
-def plan():
-    head = [("VP", 0, "diag", 0, "g")] + v_steps(0, ["sum"], "v") + [("VP", 0, "inv", 0, "v")]
-    head += [("THR", 0, 0, "v"), ("THR", 0, 1, "s"), ("THR", 1, 0, "v"), ("THR", 1, 1, "s"), ("THQ", 0)]
-    head += [("VP", 0, "scale", 0, "v"), ("VP", 0, "scale", 1, "v"), ("THQ", 1)]
-    head += [("VP", 0, "scale", 2, "v"), ("VP", 0, "scale", 3, "v")] + v_steps(0, ["fix"], "v")
-    head += [("T", 0, 0, 0, "s"), ("T", 0, 0, 1, "s"), ("QX", 0, 0), ("T", 0, 1, 0, "s"), ("T", 0, 1, 1, "s")]
-    head += [("THR", 2, 0, "v"), ("QX", 0, 1), ("THR", 2, 1, "v"), ("THQ", 2)]
-    second = [("VP", 1, "diag", 0, "g")] + [("VP", 1, "tree", i, "g") for i in range(4)]
-    second += [("VP", 1, "treesum", 3, "v"), ("VP", 1, "inv", 0, "v")] + v_steps(1, ["scale", "fix"], "g")
-    fill = {
-        (0, 0): [("THR", 3, 0, "v")],
-        (0, 1): [("THR", 3, 1, "v"), ("THQ", 3)],
-        (1, -1): [("VT", 0, 0, "s")],
-        (1, 2): [("VT", 0, 1, "s")],
-        (1, 3): [("QV", 0)],
-        (2, 0): second,
-        (4, -1): [("VT", 1, 0, "s")],
-        (4, 1): [("VT", 1, 1, "v")],
-        (4, 3): [("QV", 1)],
-    }
-    return head + body(fill, {0: "sssv", 1: "ssss"}, {0: "ss", 1: "vs"}, {0: 3, 1: 1})
+STAGE = 12
+X_OUT = "svsv"
+V_OUT = "sv"
+H_OUT = "svss"
+H_OUT_FIRST = "ssss"
+O_OUT = "svsv"
+TREE = 4
+LOADS = ("a0", "x0", "t0", "t1", "x1", "a1", "x2", "x3")
 
 
 def tile_akgcn_pa_kernel(tc, x, adj, lam_raw, theta, out):
@@ -86,10 +33,8 @@ def tile_akgcn_pa_kernel(tc, x, adj, lam_raw, theta, out):
     with ExitStack() as ctx:
         keep = ctx.enter_context(tc.tile_pool(name="keep", bufs=1))
         work = ctx.enter_context(tc.tile_pool(name="work", bufs=2))
-        stage = ctx.enter_context(tc.tile_pool(name="stage", bufs=6))
-        ps_t = ctx.enter_context(tc.psum_pool(name="ps_t", bufs=PS_BUFS[0]))
-        ps_h = ctx.enter_context(tc.psum_pool(name="ps_h", bufs=PS_BUFS[1]))
-        ps_o = ctx.enter_context(tc.psum_pool(name="ps_o", bufs=PS_BUFS[2]))
+        stage = ctx.enter_context(tc.tile_pool(name="stage", bufs=STAGE))
+        banks = ctx.enter_context(tc.psum_pool(name="banks", bufs=8))
         ctx.enter_context(tc.manual_schedule())
 
         def copy_out(engine, dst, src):
@@ -98,19 +43,11 @@ def tile_akgcn_pa_kernel(tc, x, adj, lam_raw, theta, out):
             else:
                 nc.vector.tensor_copy(out=dst, in_=src)
 
-        def times_column(engine, dst, src, column):
-            if engine == "s":
-                nc.scalar.activation(out=dst, in_=src, func=ACT.Copy, scale=column)
-            elif engine == "g":
-                nc.gpsimd.tensor_scalar(out=dst, in0=src, scalar1=column, scalar2=0.0, op0=ALU.mult, op1=ALU.add)
-            else:
-                nc.vector.tensor_scalar(out=dst, in0=src, scalar1=column, scalar2=None, op0=ALU.mult)
-
         lam_sb = keep.tile([P, 1], BF16, name="lam_sb")
         nc.scalar.dma_start(out=lam_sb[:], in_=lam_raw.partition_broadcast(P))
         adj_sb = [keep.tile([P, 5 * N], BF16, name="adj%d" % b) for b in range(B)]
         x_sb = [keep.tile([P, 4, C], BF16, name="x%d" % bt) for bt in range(B * T)]
-        th_raw = [keep.tile([P, 8, 512], BF16, name="th%d" % h) for h in range(2)]
+        th_sb = [keep.tile([P, 8, HALF], BF16, name="th%d" % h) for h in range(2)]
         for item in LOADS:
             k = int(item[1])
             if item[0] == "a":
@@ -122,9 +59,9 @@ def tile_akgcn_pa_kernel(tc, x, adj, lam_raw, theta, out):
                 nc.sync.dma_start(out=x_sb[k][:], in_=x[k // T, k % T].rearrange("(j p) c -> p j c", p=P))
             else:
                 src = theta.rearrange("(t q e) c -> q t e c", t=4, q=P, e=2)
-                dst = th_raw[k][:].rearrange("q (t e) c -> q t e c", e=2)
+                dst = th_sb[k][:].rearrange("q (t e) c -> q t e c", e=2)
                 for e in range(2):
-                    nc.sync.dma_start(out=dst[:, :, e, :], in_=src[:, :, e, 512 * k : 512 * k + 512])
+                    nc.sync.dma_start(out=dst[:, :, e, :], in_=src[:, :, e, HALF * k : HALF * k + HALF])
 
         ident_f = keep.tile([P, P], F32, name="ident_f")
         make_identity(nc, ident_f[:])
@@ -135,193 +72,192 @@ def tile_akgcn_pa_kernel(tc, x, adj, lam_raw, theta, out):
         r_eye = keep.tile([P, P], F32, name="r_eye")
         nc.vector.tensor_scalar(out=r_eye[:], in0=ident_f[:], scalar1=r[:, 0:1], scalar2=None, op0=ALU.mult)
 
-        thc = keep.tile([P, 4, 2, 256], U32, name="thc", align_bytes=64)
-        ths = keep.tile([P, 4, 2, 256], U8, name="ths", align_bytes=64)
-        vc = [keep.tile([P, N], U32, name="vc%d" % b, align_bytes=64) for b in range(B)]
-        vs = [keep.tile([P, N], U8, name="vs%d" % b, align_bytes=64) for b in range(B)]
-        vg = [keep.tile([P, N, 4], BF16, name="vg%d" % b, align_bytes=64) for b in range(B)]
-        rowsum = [keep.tile([P, 4], F32, name="rowsum%d" % b) for b in range(B)]
-        den = [keep.tile([P, 4], F32, name="den%d" % b) for b in range(B)]
-        rinv = [keep.tile([P, 4], F32, name="rinv%d" % b) for b in range(B)]
-        wdiag = [keep.tile([P, 4, P], F32, name="wdiag%d" % b) for b in range(B)]
-        vb = [keep.tile([P, 4, N], BF16, name="vb%d" % b) for b in range(B)]
-        xq = {}
-        hq = {}
-        tgs = {}
-        tree = {}
+        th_codes = keep.tile([P, 4, 2, 256], U32, name="th_codes", align_bytes=64)
+        th_scales = keep.tile([P, 4, 2, 256], U8, name="th_scales", align_bytes=64)
+        v_codes = [keep.tile([P, N], U32, name="v_codes%d" % b, align_bytes=64) for b in range(B)]
+        v_scales = [keep.tile([P, N], U8, name="v_scales%d" % b, align_bytes=64) for b in range(B)]
+        v_rows = [keep.tile([P, 4, N], BF16, name="v_rows%d" % b) for b in range(B)]
+        partial = [keep.tile([P, 4, 256 >> (TREE - 1)], F32, name="partial%d" % b) for b in range(B)]
+        with_diag = [keep.tile([P, 4, P], F32, name="with_diag%d" % b) for b in range(B)]
 
-        def v_piece(b, kind, i, engine):
+        def v_sums(b):
             rows = adj_sb[b][:, 0 : 4 * N].rearrange("p (i m) -> p i m", i=4)
-            if kind == "diag":
-                nc.gpsimd.tensor_tensor(
-                    out=wdiag[b][:],
-                    in0=adj_sb[b][:].rearrange("p (i s) -> p i s", s=N + P)[:, :, 0:P],
-                    in1=r_eye[:].unsqueeze(1).to_broadcast([P, 4, P]),
-                    op=ALU.add,
-                )
-            elif kind == "sum":
-                if engine == "s":
-                    junk = work.tile([P, N], BF16, name="junk")
-                    nc.scalar.activation(
-                        out=junk[:], in_=rows[:, i, :], func=ACT.Copy, accum_out=rowsum[b][:, i : i + 1]
-                    )
+            nc.gpsimd.tensor_tensor(
+                out=with_diag[b][:],
+                in0=adj_sb[b][:].rearrange("p (i s) -> p i s", s=N + P)[:, :, 0:P],
+                in1=r_eye[:].unsqueeze(1).to_broadcast([P, 4, P]),
+                op=ALU.add,
+            )
+            src = rows
+            for level in range(TREE):
+                width = 256 >> level
+                if level == TREE - 1:
+                    dst = partial[b]
                 else:
-                    nc.vector.tensor_reduce(
-                        out=rowsum[b][:, i : i + 1], in_=rows[:, i, :], axis=mybir.AxisListType.X, op=ALU.add
-                    )
-            elif kind == "tree":
-                width = 256 >> i
-                src = rows if i == 0 else tree[(b, i - 1)][:]
-                tree[(b, i)] = keep.tile([P, 4, width], F32, name="tree%d_%d" % (b, i))
-                nc.gpsimd.tensor_tensor(
-                    out=tree[(b, i)][:], in0=src[:, :, 0:width], in1=src[:, :, width : 2 * width], op=ALU.add
+                    dst = work.tile([P, 4, width], F32, name="tree%d" % level)
+                nc.gpsimd.tensor_tensor(out=dst[:], in0=src[:, :, 0:width], in1=src[:, :, width : 2 * width], op=ALU.add)
+                src = dst
+
+        def v_scale(b):
+            rows = adj_sb[b][:, 0 : 4 * N].rearrange("p (i m) -> p i m", i=4)
+            total = work.tile([P, 4], F32, name="total")
+            nc.vector.tensor_reduce(out=total[:], in_=partial[b][:], axis=mybir.AxisListType.X, op=ALU.add)
+            nc.vector.tensor_scalar(out=total[:], in0=total[:], scalar1=r[:, 0:1], scalar2=None, op0=ALU.add)
+            inverse = work.tile([P, 4], F32, name="inverse")
+            nc.vector.reciprocal(out=inverse[:], in_=total[:])
+            for i in range(4):
+                nc.gpsimd.tensor_scalar(
+                    out=v_rows[b][:, i, :], in0=rows[:, i, :], scalar1=inverse[:, i : i + 1], scalar2=0.0,
+                    op0=ALU.mult, op1=ALU.add,
                 )
-            elif kind == "treesum":
-                nc.vector.tensor_reduce(out=rowsum[b][:], in_=tree[(b, i)][:], axis=mybir.AxisListType.X, op=ALU.add)
-            elif kind == "inv":
-                nc.vector.tensor_scalar(
-                    out=den[b][:], in0=rowsum[b][:], scalar1=r[:, 0:1], scalar2=None, op0=ALU.add
+            for i in range(4):
+                nc.gpsimd.tensor_scalar(
+                    out=v_rows[b][:, i, P * i : P * i + P], in0=with_diag[b][:, i, :], scalar1=inverse[:, i : i + 1],
+                    scalar2=0.0, op0=ALU.mult, op1=ALU.add,
                 )
-                nc.vector.reciprocal(out=rinv[b][:], in_=den[b][:])
-            elif kind == "scale":
-                times_column(engine, vb[b][:, i, :], rows[:, i, :], rinv[b][:, i : i + 1])
-            else:
-                times_column(engine, vb[b][:, i, P * i : P * i + P], wdiag[b][:, i, :], rinv[b][:, i : i + 1])
 
-        def v_transpose(b, ip, engine):
-            vt = ps_t.tile([P, 2, 4, P], BF16, name="vt", tag="tp")
-            for i2 in range(2):
-                for j in range(4):
-                    nc.tensor.transpose(
-                        out=vt[:, i2, j, :], in_=vb[b][:, 2 * ip + i2, P * j : P * j + P], identity=ident_b[:]
-                    )
-            copy_out(
-                engine,
-                vg[b][:, 256 * ip : 256 * ip + 256, :].rearrange("p (i n) j -> p i n j", i=2),
-                vt[:].rearrange("p i j n -> p i n j"),
-            )
+        def v_transpose(b):
+            grouped = work.tile([P, N, 4], BF16, name="v_grouped", align_bytes=64)
+            for pair in range(2):
+                bank = banks.tile([P, 2, 4, P], BF16, name="v_bank", tag="bank")
+                for i in range(2):
+                    for j in range(4):
+                        nc.tensor.transpose(
+                            out=bank[:, i, j, :], in_=v_rows[b][:, 2 * pair + i, P * j : P * j + P], identity=ident_b[:]
+                        )
+                copy_out(
+                    V_OUT[pair],
+                    grouped[:, 256 * pair : 256 * pair + 256, :].rearrange("p (i n) j -> p i n j", i=2),
+                    bank[:].rearrange("p i j n -> p i n j"),
+                )
+            return grouped
 
-        def x_transpose(bt, g, jp, engine):
-            if bt not in xq:
-                gx = work.tile([P, 2, N, 4], BF16, name="gx", align_bytes=64)
-                xc = work.tile([P, 2, N], U32, name="xc", align_bytes=64)
-                xs = work.tile([P, 2, N], U8, name="xs", align_bytes=64)
-                xq[bt] = (gx, xc, xs)
-            xw = x_sb[bt][:].bitcast(F32)
-            gxw = xq[bt][0][:].bitcast(F32)
-            xt = ps_t.tile([P, 2, 256], F32, name="xt", tag="tp")
-            for jj in range(2):
-                for u in range(2):
-                    lo = 256 * g + P * u
-                    nc.tensor.transpose(
-                        out=xt[:, u, P * jj : P * jj + P], in_=xw[:, 2 * jp + jj, lo : lo + P], identity=ident_f[:]
-                    )
-            copy_out(engine, gxw[:, g, 256 * jp : 256 * jp + 256, :], xt[:].rearrange("q u m -> q m u"))
-
-        def x_quantise(bt, g):
-            gx, xc, xs = xq[bt]
+        def v_quantise(b, grouped):
             nc.vector.quantize_mx(
-                out=xc[:, g, :].bitcast(FP8X4), scales=xs[:, g, :], in_=gx[:, g].rearrange("q m t -> q (m t)")
+                out=v_codes[b][:].bitcast(FP8X4), scales=v_scales[b][:], in_=grouped[:].rearrange("p n j -> p (n j)")
             )
 
-        def theta_regroup(piece, g, engine):
-            if piece not in tgs:
-                tgs[piece] = keep.tile([P, 2, 256, 4], BF16, name="tg%d" % piece, align_bytes=64)
+        def x_transpose(bt):
+            words = x_sb[bt][:].bitcast(F32)
+            grouped = work.tile([P, 2, N, 4], BF16, name="x_grouped", align_bytes=64)
+            for g in range(2):
+                for pair in range(2):
+                    bank = banks.tile([P, 2, 256], F32, name="x_bank", tag="bank")
+                    for jj in range(2):
+                        for u in range(2):
+                            lo = 256 * g + P * u
+                            nc.tensor.transpose(
+                                out=bank[:, u, P * jj : P * jj + P],
+                                in_=words[:, 2 * pair + jj, lo : lo + P],
+                                identity=ident_f[:],
+                            )
+                    copy_out(
+                        X_OUT[2 * g + pair],
+                        grouped[:].bitcast(F32)[:, g, 256 * pair : 256 * pair + 256, :],
+                        bank[:].rearrange("q u m -> q m u"),
+                    )
+            return grouped
+
+        def x_quantise(grouped):
+            codes = work.tile([P, 2, N], U32, name="x_codes", align_bytes=64)
+            scales = work.tile([P, 2, N], U8, name="x_scales", align_bytes=64)
+            for g in range(2):
+                nc.vector.quantize_mx(
+                    out=codes[:, g, :].bitcast(FP8X4), scales=scales[:, g, :],
+                    in_=grouped[:, g].rearrange("q m t -> q (m t)"),
+                )
+            return codes, scales
+
+        def theta_piece(piece):
+            grouped = work.tile([P, 2, 256, 4], BF16, name="th_grouped", align_bytes=64)
             lo = 256 * (piece % 2)
-            dst = tgs[piece][:, g].rearrange("p (c i) t -> p c t i", i=4)
-            src = th_raw[piece // 2][:, 4 * g : 4 * g + 4, lo : lo + 256].rearrange("p t (c i) -> p c t i", i=4)
-            if engine == "g":
-                nc.gpsimd.tensor_scalar(out=dst, in0=src, scalar1=1.0, scalar2=0.0, op0=ALU.mult, op1=ALU.add)
-            else:
-                copy_out(engine, dst, src)
-
-        def theta_quantise(piece):
-            tg = tgs[piece]
+            for g in range(2):
+                copy_out(
+                    "vs"[g],
+                    grouped[:, g].rearrange("p (c i) t -> p c t i", i=4),
+                    th_sb[piece // 2][:, 4 * g : 4 * g + 4, lo : lo + 256].rearrange("p t (c i) -> p c t i", i=4),
+                )
             nc.vector.quantize_mx(
-                out=thc[:, piece].rearrange("p g c -> p (g c)").bitcast(FP8X4),
-                scales=ths[:, piece].rearrange("p g c -> p (g c)"),
-                in_=tg[:].rearrange("p g c t -> p (g c t)"),
+                out=th_codes[:, piece].rearrange("p g c -> p (g c)").bitcast(FP8X4),
+                scales=th_scales[:, piece].rearrange("p g c -> p (g c)"),
+                in_=grouped[:].rearrange("p g c t -> p (g c t)"),
             )
 
-        def first_product(bt, h, c4, engine):
-            if bt not in hq:
-                hg = work.tile([P, C, 4], BF16, name="hg", align_bytes=64)
-                hc = work.tile([P, C], U32, name="hc", align_bytes=64, bufs=3)
-                hs = work.tile([P, C], U8, name="hs", align_bytes=64, bufs=3)
-                hq[bt] = (hg, hc, hs)
-            xc, xs = xq[bt][1], xq[bt][2]
-            hp = ps_h.tile([P, 4, P], F32, name="hp")
-            piece = 2 * h + c4 // 2
-            cols = slice(P * (c4 % 2), P * (c4 % 2) + P)
+        def first_product(x_codes, x_scales, h_grouped, h, k, engine):
+            bank = banks.tile([P, 4, P], F32, name="h_bank", tag="bank")
+            piece = 2 * h + k // 2
+            cols = slice(P * (k % 2), P * (k % 2) + P)
             for j in range(4):
                 rows = slice(P * j, P * j + P)
                 for g in range(2):
                     nc.tensor.matmul_mx(
-                        out=hp[:, j, :],
-                        lhsT=xc[:, g, rows].bitcast(FP8X4),
-                        lhsT_scale=xs[:, g, rows],
-                        rhs=thc[:, piece, g, cols].bitcast(FP8X4),
-                        rhs_scale=ths[:, piece, g, cols],
+                        out=bank[:, j, :],
+                        lhsT=x_codes[:, g, rows].bitcast(FP8X4),
+                        lhsT_scale=x_scales[:, g, rows],
+                        rhs=th_codes[:, piece, g, cols].bitcast(FP8X4),
+                        rhs_scale=th_scales[:, piece, g, cols],
                         start=(g == 0),
                         stop=(g == 1),
                     )
-            lo = 512 * h + P * c4
-            copy_out(engine, hq[bt][0][:, lo : lo + P, :], hp[:].rearrange("p j c -> p c j"))
+            copy_out(engine, h_grouped[:, P * k : P * k + P, :], bank[:].rearrange("p j c -> p c j"))
 
-        def h_quantise(bt, h):
-            hg, hc, hs = hq[bt]
-            half = slice(512 * h, 512 * h + 512)
-            nc.vector.quantize_mx(
-                out=hc[:, half].bitcast(FP8X4), scales=hs[:, half], in_=hg[:, half, :].rearrange("p c j -> p (c j)")
-            )
-
-        def second_product(bt, ch, i, engine):
+        def second_product(u, h_codes, h_scales, i, engine):
+            bt, h = u // 2, u % 2
             b = bt // T
-            hc, hs = hq[bt][1], hq[bt][2]
-            half = slice(512 * ch, 512 * ch + 512)
             rows = slice(P * i, P * i + P)
-            op = ps_o.tile([P, 512], F32, name="op")
+            bank = banks.tile([P, HALF], F32, name="o_bank", tag="bank")
             nc.tensor.matmul_mx(
-                out=op[:],
-                lhsT=vc[b][:, rows].bitcast(FP8X4),
-                lhsT_scale=vs[b][:, rows],
-                rhs=hc[:, half].bitcast(FP8X4),
-                rhs_scale=hs[:, half],
+                out=bank[:],
+                lhsT=v_codes[b][:, rows].bitcast(FP8X4),
+                lhsT_scale=v_scales[b][:, rows],
+                rhs=h_codes[:].bitcast(FP8X4),
+                rhs_scale=h_scales[:],
                 start=True,
                 stop=True,
             )
-            ob = stage.tile([P, 512], F32, name="ob")
+            result = stage.tile([P, HALF], F32, name="result")
             if engine == "s":
-                nc.scalar.activation(out=ob[:], in_=op[:], func=ACT.Relu)
+                nc.scalar.activation(out=result[:], in_=bank[:], func=ACT.Relu)
             else:
-                nc.vector.tensor_scalar_max(out=ob[:], in0=op[:], scalar1=0.0)
-            nc.sync.dma_start(out=out[b, bt % T, rows, half], in_=ob[:])
+                nc.vector.tensor_scalar_max(out=result[:], in0=bank[:], scalar1=0.0)
+            nc.sync.dma_start(out=out[b, bt % T, rows, HALF * h : HALF * h + HALF], in_=result[:])
 
-        for tok in plan():
-            kind = tok[0]
-            if kind == "VP":
-                v_piece(tok[1], tok[2], tok[3], tok[4])
-            elif kind == "TH":
-                theta_regroup(tok[1], 0, tok[2][0])
-                theta_regroup(tok[1], 1, tok[2][1])
-                theta_quantise(tok[1])
-            elif kind == "THR":
-                theta_regroup(tok[1], tok[2], tok[3])
-            elif kind == "THQ":
-                theta_quantise(tok[1])
-            elif kind == "T":
-                x_transpose(tok[1], tok[2], tok[3], tok[4])
-            elif kind == "QX":
-                x_quantise(tok[1], tok[2])
-            elif kind == "VT":
-                v_transpose(tok[1], tok[2], tok[3])
-            elif kind == "QV":
+        v_sums(0)
+        x_now = x_quantise(x_transpose(0))
+        theta_piece(0)
+        theta_piece(1)
+        v_scale(0)
+        h_done = []
+        for u in range(UNITS + LAG):
+            bt, h = u // 2, u % 2
+            if u < UNITS:
+                if h == 0 and u > 0:
+                    x_now = x_next
+                if h == 1 and bt + 1 < B * T:
+                    x_grouped = x_transpose(bt + 1)
+                    if bt % T == 0:
+                        v_grouped = v_transpose(bt // T)
+                h_grouped = work.tile([P, HALF, 4], BF16, name="h_grouped", align_bytes=64)
+            if u == 2:
+                v_sums(1)
+            if u == 3:
+                v_scale(1)
+            for k in range(4):
+                if u < UNITS:
+                    if u == 0 and k % 2 == 0:
+                        theta_piece(2 + k // 2)
+                    first_product(x_now[0], x_now[1], h_grouped, h, k, (H_OUT_FIRST if bt == 0 else H_OUT)[k])
+                if u >= LAG:
+                    second_product(u - LAG, h_done[u - LAG][0], h_done[u - LAG][1], k, O_OUT[k])
+                if u < UNITS and h == 1 and bt + 1 < B * T:
+                    if k == 0:
+                        x_next = x_quantise(x_grouped)
+                    if k == 1 and bt % T == 0:
+                        v_quantise(bt // T, v_grouped)
+            if u < UNITS:
+                h_codes = work.tile([P, HALF], U32, name="h_codes", align_bytes=64, bufs=LAG + 2)
+                h_scales = work.tile([P, HALF], U8, name="h_scales", align_bytes=64, bufs=LAG + 2)
                 nc.vector.quantize_mx(
-                    out=vc[tok[1]][:].bitcast(FP8X4), scales=vs[tok[1]][:], in_=vg[tok[1]][:].rearrange("p n j -> p (n j)")
+                    out=h_codes[:].bitcast(FP8X4), scales=h_scales[:], in_=h_grouped[:].rearrange("p c j -> p (c j)")
                 )
-            elif kind == "S1":
-                first_product(tok[1], tok[2], tok[3], tok[4])
-            elif kind == "QH":
-                h_quantise(tok[1], tok[2])
-            else:
-                second_product(tok[1], tok[2], tok[3], tok[4])
+                h_done.append((h_codes, h_scales))

@@ -17,7 +17,7 @@ FLOPS = 2 * B * T * N * C * C + 2 * B * T * N * N * C
 
 HALF = 512
 UNITS = 2 * B * T
-LAG = 2
+LAG = 8
 STAGE = 12
 X_OUT = "svsv"
 V_OUT = "sv"
@@ -25,7 +25,7 @@ H_OUT = "svss"
 H_OUT_FIRST = "ssss"
 O_OUT = "svsv"
 TREE = 4
-LOADS = ("a0", "x0", "t0", "t1", "x1", "a1", "x2", "x3")
+LOADS = ("a0", "x0", "t0", "t1", "t2", "t3", "x1", "a1", "x2", "x3")
 
 
 def tile_akgcn_pa_kernel(tc, x, adj, lam_raw, theta, out):
@@ -47,7 +47,7 @@ def tile_akgcn_pa_kernel(tc, x, adj, lam_raw, theta, out):
         nc.scalar.dma_start(out=lam_sb[:], in_=lam_raw.partition_broadcast(P))
         adj_sb = [keep.tile([P, 5 * N], BF16, name="adj%d" % b) for b in range(B)]
         x_sb = [keep.tile([P, 4, C], BF16, name="x%d" % bt) for bt in range(B * T)]
-        th_sb = [keep.tile([P, 8, HALF], BF16, name="th%d" % h) for h in range(2)]
+        th_sb = [keep.tile([P, 8, 256], BF16, name="th%d" % piece) for piece in range(4)]
         for item in LOADS:
             k = int(item[1])
             if item[0] == "a":
@@ -56,12 +56,14 @@ def tile_akgcn_pa_kernel(tc, x, adj, lam_raw, theta, out):
                     in_=adj[k].rearrange("(i p) m -> p i m", p=P),
                 )
             elif item[0] == "x":
-                nc.sync.dma_start(out=x_sb[k][:], in_=x[k // T, k % T].rearrange("(j p) c -> p j c", p=P))
+                src = x[k // T, k % T].rearrange("(j p) c -> p j c", p=P)
+                for pair in range(2):
+                    nc.sync.dma_start(out=x_sb[k][:, 2 * pair : 2 * pair + 2, :], in_=src[:, 2 * pair : 2 * pair + 2, :])
             else:
                 src = theta.rearrange("(t q e) c -> q t e c", t=4, q=P, e=2)
                 dst = th_sb[k][:].rearrange("q (t e) c -> q t e c", e=2)
                 for e in range(2):
-                    nc.sync.dma_start(out=dst[:, :, e, :], in_=src[:, :, e, HALF * k : HALF * k + HALF])
+                    nc.sync.dma_start(out=dst[:, :, e, :], in_=src[:, :, e, 256 * k : 256 * k + 256])
 
         ident_f = keep.tile([P, P], F32, name="ident_f")
         make_identity(nc, ident_f[:])
@@ -80,9 +82,9 @@ def tile_akgcn_pa_kernel(tc, x, adj, lam_raw, theta, out):
         partial = [keep.tile([P, 4, 256 >> (TREE - 1)], F32, name="partial%d" % b) for b in range(B)]
         with_diag = [keep.tile([P, 4, P], F32, name="with_diag%d" % b) for b in range(B)]
 
-        def v_sums(b):
+        def v_sums(b, engine):
             rows = adj_sb[b][:, 0 : 4 * N].rearrange("p (i m) -> p i m", i=4)
-            nc.gpsimd.tensor_tensor(
+            engine.tensor_tensor(
                 out=with_diag[b][:],
                 in0=adj_sb[b][:].rearrange("p (i s) -> p i s", s=N + P)[:, :, 0:P],
                 in1=r_eye[:].unsqueeze(1).to_broadcast([P, 4, P]),
@@ -95,10 +97,10 @@ def tile_akgcn_pa_kernel(tc, x, adj, lam_raw, theta, out):
                     dst = partial[b]
                 else:
                     dst = work.tile([P, 4, width], F32, name="tree%d" % level)
-                nc.gpsimd.tensor_tensor(out=dst[:], in0=src[:, :, 0:width], in1=src[:, :, width : 2 * width], op=ALU.add)
+                engine.tensor_tensor(out=dst[:], in0=src[:, :, 0:width], in1=src[:, :, width : 2 * width], op=ALU.add)
                 src = dst
 
-        def v_scale(b):
+        def v_scale(b, engine):
             rows = adj_sb[b][:, 0 : 4 * N].rearrange("p (i m) -> p i m", i=4)
             total = work.tile([P, 4], F32, name="total")
             nc.vector.tensor_reduce(out=total[:], in_=partial[b][:], axis=mybir.AxisListType.X, op=ALU.add)
@@ -106,12 +108,12 @@ def tile_akgcn_pa_kernel(tc, x, adj, lam_raw, theta, out):
             inverse = work.tile([P, 4], F32, name="inverse")
             nc.vector.reciprocal(out=inverse[:], in_=total[:])
             for i in range(4):
-                nc.gpsimd.tensor_scalar(
+                engine.tensor_scalar(
                     out=v_rows[b][:, i, :], in0=rows[:, i, :], scalar1=inverse[:, i : i + 1], scalar2=0.0,
                     op0=ALU.mult, op1=ALU.add,
                 )
             for i in range(4):
-                nc.gpsimd.tensor_scalar(
+                engine.tensor_scalar(
                     out=v_rows[b][:, i, P * i : P * i + P], in0=with_diag[b][:, i, :], scalar1=inverse[:, i : i + 1],
                     scalar2=0.0, op0=ALU.mult, op1=ALU.add,
                 )
@@ -140,8 +142,8 @@ def tile_akgcn_pa_kernel(tc, x, adj, lam_raw, theta, out):
         def x_transpose(bt):
             words = x_sb[bt][:].bitcast(F32)
             grouped = work.tile([P, 2, N, 4], BF16, name="x_grouped", align_bytes=64)
-            for g in range(2):
-                for pair in range(2):
+            for pair in range(2):
+                for g in range(2):
                     bank = banks.tile([P, 2, 256], F32, name="x_bank", tag="bank")
                     for jj in range(2):
                         for u in range(2):
@@ -152,7 +154,7 @@ def tile_akgcn_pa_kernel(tc, x, adj, lam_raw, theta, out):
                                 identity=ident_f[:],
                             )
                     copy_out(
-                        X_OUT[2 * g + pair],
+                        X_OUT[2 * pair + g],
                         grouped[:].bitcast(F32)[:, g, 256 * pair : 256 * pair + 256, :],
                         bank[:].rearrange("q u m -> q m u"),
                     )
@@ -170,12 +172,11 @@ def tile_akgcn_pa_kernel(tc, x, adj, lam_raw, theta, out):
 
         def theta_piece(piece):
             grouped = work.tile([P, 2, 256, 4], BF16, name="th_grouped", align_bytes=64)
-            lo = 256 * (piece % 2)
             for g in range(2):
                 copy_out(
                     "vs"[g],
                     grouped[:, g].rearrange("p (c i) t -> p c t i", i=4),
-                    th_sb[piece // 2][:, 4 * g : 4 * g + 4, lo : lo + 256].rearrange("p t (c i) -> p c t i", i=4),
+                    th_sb[piece][:, 4 * g : 4 * g + 4, :].rearrange("p t (c i) -> p c t i", i=4),
                 )
             nc.vector.quantize_mx(
                 out=th_codes[:, piece].rearrange("p g c -> p (g c)").bitcast(FP8X4),
@@ -222,42 +223,45 @@ def tile_akgcn_pa_kernel(tc, x, adj, lam_raw, theta, out):
                 nc.vector.tensor_scalar_max(out=result[:], in0=bank[:], scalar1=0.0)
             nc.sync.dma_start(out=out[b, bt % T, rows, HALF * h : HALF * h + HALF], in_=result[:])
 
-        v_sums(0)
+        v_sums(0, nc.vector)
+        v_scale(0, nc.vector)
         x_now = x_quantise(x_transpose(0))
         theta_piece(0)
         theta_piece(1)
-        v_scale(0)
+        v_quantise(0, v_transpose(0))
         h_done = []
-        for u in range(UNITS + LAG):
-            bt, h = u // 2, u % 2
+        for n in range(4 * UNITS + LAG):
+            u, k = divmod(n, 4)
+            bt, h = divmod(u, 2)
             if u < UNITS:
-                if h == 0 and u > 0:
-                    x_now = x_next
-                if h == 1 and bt + 1 < B * T:
-                    x_grouped = x_transpose(bt + 1)
-                    if bt % T == 0:
-                        v_grouped = v_transpose(bt // T)
-                h_grouped = work.tile([P, HALF, 4], BF16, name="h_grouped", align_bytes=64)
-            if u == 2:
-                v_sums(1)
-            if u == 3:
-                v_scale(1)
-            for k in range(4):
-                if u < UNITS:
-                    if u == 0 and k % 2 == 0:
-                        theta_piece(2 + k // 2)
-                    first_product(x_now[0], x_now[1], h_grouped, h, k, (H_OUT_FIRST if bt == 0 else H_OUT)[k])
-                if u >= LAG:
-                    second_product(u - LAG, h_done[u - LAG][0], h_done[u - LAG][1], k, O_OUT[k])
-                if u < UNITS and h == 1 and bt + 1 < B * T:
-                    if k == 0:
-                        x_next = x_quantise(x_grouped)
-                    if k == 1 and bt % T == 0:
-                        v_quantise(bt // T, v_grouped)
+                turn = h == 1 and bt + 1 < B * T
+                if k == 0:
+                    if h == 0 and u > 0:
+                        x_now = x_next
+                    if turn:
+                        x_grouped = x_transpose(bt + 1)
+                        if bt == T:
+                            v_grouped = v_transpose(1)
+                    h_grouped = work.tile([P, HALF, 4], BF16, name="h_grouped", align_bytes=64)
+                    if u == 2:
+                        v_sums(1, nc.gpsimd)
+                    if u == 3:
+                        v_scale(1, nc.gpsimd)
+                if u == 0 and k % 2 == 0:
+                    theta_piece(2 + k // 2)
+                first_product(x_now[0], x_now[1], h_grouped, h, k, (H_OUT_FIRST if bt == 0 else H_OUT)[k])
+            if n >= LAG:
+                w, i = divmod(n - LAG, 4)
+                second_product(w, h_done[w][0], h_done[w][1], i, O_OUT[i])
             if u < UNITS:
-                h_codes = work.tile([P, HALF], U32, name="h_codes", align_bytes=64, bufs=LAG + 2)
-                h_scales = work.tile([P, HALF], U8, name="h_scales", align_bytes=64, bufs=LAG + 2)
-                nc.vector.quantize_mx(
-                    out=h_codes[:].bitcast(FP8X4), scales=h_scales[:], in_=h_grouped[:].rearrange("p c j -> p (c j)")
-                )
-                h_done.append((h_codes, h_scales))
+                if turn and k == 0:
+                    x_next = x_quantise(x_grouped)
+                if turn and k == 1 and bt == T:
+                    v_quantise(1, v_grouped)
+                if k == 3:
+                    h_codes = work.tile([P, HALF], U32, name="h_codes", align_bytes=64, bufs=4)
+                    h_scales = work.tile([P, HALF], U8, name="h_scales", align_bytes=64, bufs=4)
+                    nc.vector.quantize_mx(
+                        out=h_codes[:].bitcast(FP8X4), scales=h_scales[:], in_=h_grouped[:].rearrange("p c j -> p (c j)")
+                    )
+                    h_done.append((h_codes, h_scales))

@@ -19,7 +19,9 @@ HALF = 512
 UNITS = 2 * B * T
 LAG = 8
 STAGE = 12
+V1_SCALE_AT = 8
 X_OUT = "svsv"
+X_OUT_FIRST = "ssss"
 V_OUT = "sv"
 H_OUT = "svss"
 H_OUT_FIRST = "ssss"
@@ -140,6 +142,7 @@ def tile_akgcn_pa_kernel(tc, x, adj, lam_raw, theta, out):
             )
 
         def x_transpose(bt):
+            engines = X_OUT_FIRST if bt == 0 else X_OUT
             words = x_sb[bt][:].bitcast(F32)
             grouped = work.tile([P, 2, N, 4], BF16, name="x_grouped", align_bytes=64)
             for pair in range(2):
@@ -154,7 +157,7 @@ def tile_akgcn_pa_kernel(tc, x, adj, lam_raw, theta, out):
                                 identity=ident_f[:],
                             )
                     copy_out(
-                        X_OUT[2 * pair + g],
+                        engines[2 * pair + g],
                         grouped[:].bitcast(F32)[:, g, 256 * pair : 256 * pair + 256, :],
                         bank[:].rearrange("q u m -> q m u"),
                     )
@@ -223,12 +226,12 @@ def tile_akgcn_pa_kernel(tc, x, adj, lam_raw, theta, out):
                 nc.vector.tensor_scalar_max(out=result[:], in0=bank[:], scalar1=0.0)
             nc.sync.dma_start(out=out[b, bt % T, rows, HALF * h : HALF * h + HALF], in_=result[:])
 
-        v_sums(0, nc.vector)
-        v_scale(0, nc.vector)
+        v_sums(0, nc.gpsimd)
         x_now = x_quantise(x_transpose(0))
+        v_scale(0, nc.gpsimd)
+        v_sums(1, nc.gpsimd)
         theta_piece(0)
         theta_piece(1)
-        v_quantise(0, v_transpose(0))
         h_done = []
         for n in range(4 * UNITS + LAG):
             u, k = divmod(n, 4)
@@ -240,13 +243,9 @@ def tile_akgcn_pa_kernel(tc, x, adj, lam_raw, theta, out):
                         x_now = x_next
                     if turn:
                         x_grouped = x_transpose(bt + 1)
-                        if bt == T:
-                            v_grouped = v_transpose(1)
+                        if bt < B:
+                            v_grouped = v_transpose(bt)
                     h_grouped = work.tile([P, HALF, 4], BF16, name="h_grouped", align_bytes=64)
-                    if u == 2:
-                        v_sums(1, nc.gpsimd)
-                    if u == 3:
-                        v_scale(1, nc.gpsimd)
                 if u == 0 and k % 2 == 0:
                     theta_piece(2 + k // 2)
                 first_product(x_now[0], x_now[1], h_grouped, h, k, (H_OUT_FIRST if bt == 0 else H_OUT)[k])
@@ -256,8 +255,10 @@ def tile_akgcn_pa_kernel(tc, x, adj, lam_raw, theta, out):
             if u < UNITS:
                 if turn and k == 0:
                     x_next = x_quantise(x_grouped)
-                if turn and k == 1 and bt == T:
-                    v_quantise(1, v_grouped)
+                if turn and k == 1 and bt < B:
+                    v_quantise(bt, v_grouped)
+                if n == V1_SCALE_AT:
+                    v_scale(1, nc.gpsimd)
                 if k == 3:
                     h_codes = work.tile([P, HALF], U32, name="h_codes", align_bytes=64, bufs=4)
                     h_scales = work.tile([P, HALF], U8, name="h_scales", align_bytes=64, bufs=4)

@@ -19,9 +19,7 @@ HALF = 512
 UNITS = 2 * B * T
 LAG = 8
 STAGE = 12
-V1_SCALE_AT = 8
 X_OUT = "svsv"
-X_OUT_FIRST = "ssss"
 V_OUT = "sv"
 H_OUT = "svss"
 H_OUT_FIRST = "ssss"
@@ -142,7 +140,6 @@ def tile_akgcn_pa_kernel(tc, x, adj, lam_raw, theta, out):
             )
 
         def x_transpose(bt):
-            engines = X_OUT_FIRST if bt == 0 else X_OUT
             words = x_sb[bt][:].bitcast(F32)
             grouped = work.tile([P, 2, N, 4], BF16, name="x_grouped", align_bytes=64)
             for pair in range(2):
@@ -157,7 +154,7 @@ def tile_akgcn_pa_kernel(tc, x, adj, lam_raw, theta, out):
                                 identity=ident_f[:],
                             )
                     copy_out(
-                        engines[2 * pair + g],
+                        X_OUT[2 * pair + g],
                         grouped[:].bitcast(F32)[:, g, 256 * pair : 256 * pair + 256, :],
                         bank[:].rearrange("q u m -> q m u"),
                     )
@@ -228,10 +225,9 @@ def tile_akgcn_pa_kernel(tc, x, adj, lam_raw, theta, out):
 
         v_sums(0, nc.gpsimd)
         x_now = x_quantise(x_transpose(0))
-        v_scale(0, nc.gpsimd)
-        v_sums(1, nc.gpsimd)
         theta_piece(0)
         theta_piece(1)
+        v_scale(0, nc.gpsimd)
         h_done = []
         for n in range(4 * UNITS + LAG):
             u, k = divmod(n, 4)
@@ -243,9 +239,13 @@ def tile_akgcn_pa_kernel(tc, x, adj, lam_raw, theta, out):
                         x_now = x_next
                     if turn:
                         x_grouped = x_transpose(bt + 1)
-                        if bt < B:
-                            v_grouped = v_transpose(bt)
+                        if bt % T == 0:
+                            v_grouped = v_transpose(bt // T)
                     h_grouped = work.tile([P, HALF, 4], BF16, name="h_grouped", align_bytes=64)
+                    if u == 2:
+                        v_sums(1, nc.gpsimd)
+                    if u == 3:
+                        v_scale(1, nc.gpsimd)
                 if u == 0 and k % 2 == 0:
                     theta_piece(2 + k // 2)
                 first_product(x_now[0], x_now[1], h_grouped, h, k, (H_OUT_FIRST if bt == 0 else H_OUT)[k])
@@ -255,10 +255,8 @@ def tile_akgcn_pa_kernel(tc, x, adj, lam_raw, theta, out):
             if u < UNITS:
                 if turn and k == 0:
                     x_next = x_quantise(x_grouped)
-                if turn and k == 1 and bt < B:
-                    v_quantise(bt, v_grouped)
-                if n == V1_SCALE_AT:
-                    v_scale(1, nc.gpsimd)
+                if turn and k == 1 and bt % T == 0:
+                    v_quantise(bt // T, v_grouped)
                 if k == 3:
                     h_codes = work.tile([P, HALF], U32, name="h_codes", align_bytes=64, bufs=4)
                     h_scales = work.tile([P, HALF], U8, name="h_scales", align_bytes=64, bufs=4)

@@ -20,11 +20,11 @@ UNITS = 2 * B * T
 LAG = 8
 STAGE = 12
 X_OUT = "svsv"
+X_OUT_FIRST = "ssss"
 V_OUT = "sv"
-H_OUT = "svss"
+H_OUT = "ssss"
 H_OUT_FIRST = "ssss"
 O_OUT = "svsv"
-TREE = 4
 LOADS = ("a0", "x0", "t0", "t1", "t2", "t3", "x1", "a1", "x2", "x3")
 
 
@@ -79,43 +79,31 @@ def tile_akgcn_pa_kernel(tc, x, adj, lam_raw, theta, out):
         v_codes = [keep.tile([P, N], U32, name="v_codes%d" % b, align_bytes=64) for b in range(B)]
         v_scales = [keep.tile([P, N], U8, name="v_scales%d" % b, align_bytes=64) for b in range(B)]
         v_rows = [keep.tile([P, 4, N], BF16, name="v_rows%d" % b) for b in range(B)]
-        partial = [keep.tile([P, 4, 256 >> (TREE - 1)], F32, name="partial%d" % b) for b in range(B)]
+        inverse = [keep.tile([P, 4], F32, name="inverse%d" % b) for b in range(B)]
         with_diag = [keep.tile([P, 4, P], F32, name="with_diag%d" % b) for b in range(B)]
 
-        def v_sums(b, engine):
+        def v_sums(b):
             rows = adj_sb[b][:, 0 : 4 * N].rearrange("p (i m) -> p i m", i=4)
-            engine.tensor_tensor(
+            nc.vector.tensor_reduce(out=inverse[b][:], in_=rows, axis=mybir.AxisListType.X, op=ALU.add)
+            nc.vector.tensor_scalar(out=inverse[b][:], in0=inverse[b][:], scalar1=r[:, 0:1], scalar2=None, op0=ALU.add)
+            nc.vector.reciprocal(out=inverse[b][:], in_=inverse[b][:])
+            nc.vector.tensor_tensor(
                 out=with_diag[b][:],
                 in0=adj_sb[b][:].rearrange("p (i s) -> p i s", s=N + P)[:, :, 0:P],
                 in1=r_eye[:].unsqueeze(1).to_broadcast([P, 4, P]),
                 op=ALU.add,
             )
-            src = rows
-            for level in range(TREE):
-                width = 256 >> level
-                if level == TREE - 1:
-                    dst = partial[b]
-                else:
-                    dst = work.tile([P, 4, width], F32, name="tree%d" % level)
-                engine.tensor_tensor(out=dst[:], in0=src[:, :, 0:width], in1=src[:, :, width : 2 * width], op=ALU.add)
-                src = dst
 
-        def v_scale(b, engine):
+        def v_scale(b):
             rows = adj_sb[b][:, 0 : 4 * N].rearrange("p (i m) -> p i m", i=4)
-            total = work.tile([P, 4], F32, name="total")
-            nc.vector.tensor_reduce(out=total[:], in_=partial[b][:], axis=mybir.AxisListType.X, op=ALU.add)
-            nc.vector.tensor_scalar(out=total[:], in0=total[:], scalar1=r[:, 0:1], scalar2=None, op0=ALU.add)
-            inverse = work.tile([P, 4], F32, name="inverse")
-            nc.vector.reciprocal(out=inverse[:], in_=total[:])
             for i in range(4):
-                engine.tensor_scalar(
-                    out=v_rows[b][:, i, :], in0=rows[:, i, :], scalar1=inverse[:, i : i + 1], scalar2=0.0,
-                    op0=ALU.mult, op1=ALU.add,
+                nc.vector.tensor_scalar(
+                    out=v_rows[b][:, i, :], in0=rows[:, i, :], scalar1=inverse[b][:, i : i + 1], scalar2=None, op0=ALU.mult
                 )
             for i in range(4):
-                engine.tensor_scalar(
-                    out=v_rows[b][:, i, P * i : P * i + P], in0=with_diag[b][:, i, :], scalar1=inverse[:, i : i + 1],
-                    scalar2=0.0, op0=ALU.mult, op1=ALU.add,
+                nc.vector.tensor_scalar(
+                    out=v_rows[b][:, i, P * i : P * i + P], in0=with_diag[b][:, i, :], scalar1=inverse[b][:, i : i + 1],
+                    scalar2=None, op0=ALU.mult,
                 )
 
         def v_transpose(b):
@@ -140,6 +128,7 @@ def tile_akgcn_pa_kernel(tc, x, adj, lam_raw, theta, out):
             )
 
         def x_transpose(bt):
+            engines = X_OUT_FIRST if bt == 0 else X_OUT
             words = x_sb[bt][:].bitcast(F32)
             grouped = work.tile([P, 2, N, 4], BF16, name="x_grouped", align_bytes=64)
             for pair in range(2):
@@ -154,7 +143,7 @@ def tile_akgcn_pa_kernel(tc, x, adj, lam_raw, theta, out):
                                 identity=ident_f[:],
                             )
                     copy_out(
-                        X_OUT[2 * pair + g],
+                        engines[2 * pair + g],
                         grouped[:].bitcast(F32)[:, g, 256 * pair : 256 * pair + 256, :],
                         bank[:].rearrange("q u m -> q m u"),
                     )
@@ -223,11 +212,12 @@ def tile_akgcn_pa_kernel(tc, x, adj, lam_raw, theta, out):
                 nc.vector.tensor_scalar_max(out=result[:], in0=bank[:], scalar1=0.0)
             nc.sync.dma_start(out=out[b, bt % T, rows, HALF * h : HALF * h + HALF], in_=result[:])
 
-        v_sums(0, nc.gpsimd)
+        v_sums(0)
+        v_scale(0)
         x_now = x_quantise(x_transpose(0))
         theta_piece(0)
         theta_piece(1)
-        v_scale(0, nc.gpsimd)
+        v_quantise(0, v_transpose(0))
         h_done = []
         for n in range(4 * UNITS + LAG):
             u, k = divmod(n, 4)
@@ -239,13 +229,13 @@ def tile_akgcn_pa_kernel(tc, x, adj, lam_raw, theta, out):
                         x_now = x_next
                     if turn:
                         x_grouped = x_transpose(bt + 1)
-                        if bt % T == 0:
-                            v_grouped = v_transpose(bt // T)
+                        if bt == T:
+                            v_grouped = v_transpose(1)
                     h_grouped = work.tile([P, HALF, 4], BF16, name="h_grouped", align_bytes=64)
                     if u == 2:
-                        v_sums(1, nc.gpsimd)
+                        v_sums(1)
                     if u == 3:
-                        v_scale(1, nc.gpsimd)
+                        v_scale(1)
                 if u == 0 and k % 2 == 0:
                     theta_piece(2 + k // 2)
                 first_product(x_now[0], x_now[1], h_grouped, h, k, (H_OUT_FIRST if bt == 0 else H_OUT)[k])
@@ -255,8 +245,8 @@ def tile_akgcn_pa_kernel(tc, x, adj, lam_raw, theta, out):
             if u < UNITS:
                 if turn and k == 0:
                     x_next = x_quantise(x_grouped)
-                if turn and k == 1 and bt % T == 0:
-                    v_quantise(bt // T, v_grouped)
+                if turn and k == 1 and bt == T:
+                    v_quantise(1, v_grouped)
                 if k == 3:
                     h_codes = work.tile([P, HALF], U32, name="h_codes", align_bytes=64, bufs=4)
                     h_scales = work.tile([P, HALF], U8, name="h_scales", align_bytes=64, bufs=4)

@@ -9,23 +9,16 @@ U32 = mybir.dt.uint32
 U8 = mybir.dt.uint8
 FP8X4 = mybir.dt.float8_e4m3fn_x4
 ALU = mybir.AluOpType
-ACT = mybir.ActivationFunctionType
 
 P = 128
 B, T, N, C = 2, 2, 512, 1024
 FLOPS = 2 * B * T * N * C * C + 2 * B * T * N * N * C
 
-HALF = 512
-UNITS = 2 * B * T
+SLABS = B * T
+HALF = C // 2
+PIECE = C // 4
+BANKS = 8 * SLABS
 LAG = 8
-STAGE = 12
-X_OUT = "svsv"
-X_OUT_FIRST = "ssss"
-V_OUT = "sv"
-H_OUT = "ssss"
-H_OUT_FIRST = "ssss"
-O_OUT = "svsv"
-LOADS = ("a0", "x0", "t0", "t1", "t2", "t3", "x1", "a1", "x2", "x3")
 
 
 def tile_akgcn_pa_kernel(tc, x, adj, lam_raw, theta, out):
@@ -33,37 +26,47 @@ def tile_akgcn_pa_kernel(tc, x, adj, lam_raw, theta, out):
     with ExitStack() as ctx:
         keep = ctx.enter_context(tc.tile_pool(name="keep", bufs=1))
         work = ctx.enter_context(tc.tile_pool(name="work", bufs=2))
-        stage = ctx.enter_context(tc.tile_pool(name="stage", bufs=STAGE))
+        stage = ctx.enter_context(tc.tile_pool(name="stage", bufs=12))
         banks = ctx.enter_context(tc.psum_pool(name="banks", bufs=8))
         ctx.enter_context(tc.manual_schedule())
 
-        def copy_out(engine, dst, src):
-            if engine == "s":
+        def copy_out(turn, dst, src):
+            if turn % 2 == 0:
                 nc.scalar.copy(out=dst, in_=src)
             else:
                 nc.vector.tensor_copy(out=dst, in_=src)
 
         lam_sb = keep.tile([P, 1], BF16, name="lam_sb")
-        nc.scalar.dma_start(out=lam_sb[:], in_=lam_raw.partition_broadcast(P))
         adj_sb = [keep.tile([P, 5 * N], BF16, name="adj%d" % b) for b in range(B)]
-        x_sb = [keep.tile([P, 4, C], BF16, name="x%d" % bt) for bt in range(B * T)]
-        th_sb = [keep.tile([P, 8, 256], BF16, name="th%d" % piece) for piece in range(4)]
-        for item in LOADS:
-            k = int(item[1])
-            if item[0] == "a":
-                nc.sync.dma_start(
-                    out=adj_sb[k][:, 0 : 4 * N].rearrange("p (i m) -> p i m", i=4),
-                    in_=adj[k].rearrange("(i p) m -> p i m", p=P),
-                )
-            elif item[0] == "x":
-                src = x[k // T, k % T].rearrange("(j p) c -> p j c", p=P)
-                for pair in range(2):
-                    nc.sync.dma_start(out=x_sb[k][:, 2 * pair : 2 * pair + 2, :], in_=src[:, 2 * pair : 2 * pair + 2, :])
-            else:
-                src = theta.rearrange("(t q e) c -> q t e c", t=4, q=P, e=2)
-                dst = th_sb[k][:].rearrange("q (t e) c -> q t e c", e=2)
-                for e in range(2):
-                    nc.sync.dma_start(out=dst[:, :, e, :], in_=src[:, :, e, 256 * k : 256 * k + 256])
+        x_sb = [keep.tile([P, 4, C], BF16, name="x%d" % s) for s in range(SLABS)]
+        th_sb = [keep.tile([P, 8, PIECE], BF16, name="th%d" % piece) for piece in range(4)]
+
+        def load_adj(b):
+            nc.sync.dma_start(
+                out=adj_sb[b][:, 0 : 4 * N].rearrange("p (i m) -> p i m", i=4),
+                in_=adj[b].rearrange("(i p) m -> p i m", p=P),
+            )
+
+        def load_x(s):
+            rows = x[s // T, s % T].rearrange("(j p) c -> p j c", p=P)
+            for pair in range(2):
+                nc.sync.dma_start(out=x_sb[s][:, 2 * pair : 2 * pair + 2, :], in_=rows[:, 2 * pair : 2 * pair + 2, :])
+
+        def load_theta(piece):
+            src = theta.rearrange("(t q e) c -> q t e c", t=4, q=P, e=2)
+            dst = th_sb[piece][:].rearrange("q (t e) c -> q t e c", e=2)
+            for e in range(2):
+                nc.sync.dma_start(out=dst[:, :, e, :], in_=src[:, :, e, PIECE * piece : PIECE * piece + PIECE])
+
+        nc.scalar.dma_start(out=lam_sb[:], in_=lam_raw.partition_broadcast(P))
+        load_adj(0)
+        load_x(0)
+        for piece in range(4):
+            load_theta(piece)
+        load_x(1)
+        load_adj(1)
+        load_x(2)
+        load_x(3)
 
         ident_f = keep.tile([P, P], F32, name="ident_f")
         make_identity(nc, ident_f[:])
@@ -74,8 +77,8 @@ def tile_akgcn_pa_kernel(tc, x, adj, lam_raw, theta, out):
         r_eye = keep.tile([P, P], F32, name="r_eye")
         nc.vector.tensor_scalar(out=r_eye[:], in0=ident_f[:], scalar1=r[:, 0:1], scalar2=None, op0=ALU.mult)
 
-        th_codes = keep.tile([P, 4, 2, 256], U32, name="th_codes", align_bytes=64)
-        th_scales = keep.tile([P, 4, 2, 256], U8, name="th_scales", align_bytes=64)
+        th_codes = keep.tile([P, 4, 2, PIECE], U32, name="th_codes", align_bytes=64)
+        th_scales = keep.tile([P, 4, 2, PIECE], U8, name="th_scales", align_bytes=64)
         v_codes = [keep.tile([P, N], U32, name="v_codes%d" % b, align_bytes=64) for b in range(B)]
         v_scales = [keep.tile([P, N], U8, name="v_scales%d" % b, align_bytes=64) for b in range(B)]
         v_rows = [keep.tile([P, 4, N], BF16, name="v_rows%d" % b) for b in range(B)]
@@ -102,8 +105,11 @@ def tile_akgcn_pa_kernel(tc, x, adj, lam_raw, theta, out):
                 )
             for i in range(4):
                 nc.vector.tensor_scalar(
-                    out=v_rows[b][:, i, P * i : P * i + P], in0=with_diag[b][:, i, :], scalar1=inverse[b][:, i : i + 1],
-                    scalar2=None, op0=ALU.mult,
+                    out=v_rows[b][:, i, P * i : P * i + P],
+                    in0=with_diag[b][:, i, :],
+                    scalar1=inverse[b][:, i : i + 1],
+                    scalar2=None,
+                    op0=ALU.mult,
                 )
 
         def v_transpose(b):
@@ -116,7 +122,7 @@ def tile_akgcn_pa_kernel(tc, x, adj, lam_raw, theta, out):
                             out=bank[:, i, j, :], in_=v_rows[b][:, 2 * pair + i, P * j : P * j + P], identity=ident_b[:]
                         )
                 copy_out(
-                    V_OUT[pair],
+                    pair,
                     grouped[:, 256 * pair : 256 * pair + 256, :].rearrange("p (i n) j -> p i n j", i=2),
                     bank[:].rearrange("p i j n -> p i n j"),
                 )
@@ -127,9 +133,8 @@ def tile_akgcn_pa_kernel(tc, x, adj, lam_raw, theta, out):
                 out=v_codes[b][:].bitcast(FP8X4), scales=v_scales[b][:], in_=grouped[:].rearrange("p n j -> p (n j)")
             )
 
-        def x_transpose(bt):
-            engines = X_OUT_FIRST if bt == 0 else X_OUT
-            words = x_sb[bt][:].bitcast(F32)
+        def x_transpose(s):
+            words = x_sb[s][:].bitcast(F32)
             grouped = work.tile([P, 2, N, 4], BF16, name="x_grouped", align_bytes=64)
             for pair in range(2):
                 for g in range(2):
@@ -143,7 +148,7 @@ def tile_akgcn_pa_kernel(tc, x, adj, lam_raw, theta, out):
                                 identity=ident_f[:],
                             )
                     copy_out(
-                        engines[2 * pair + g],
+                        g,
                         grouped[:].bitcast(F32)[:, g, 256 * pair : 256 * pair + 256, :],
                         bank[:].rearrange("q u m -> q m u"),
                     )
@@ -154,16 +159,17 @@ def tile_akgcn_pa_kernel(tc, x, adj, lam_raw, theta, out):
             scales = work.tile([P, 2, N], U8, name="x_scales", align_bytes=64)
             for g in range(2):
                 nc.vector.quantize_mx(
-                    out=codes[:, g, :].bitcast(FP8X4), scales=scales[:, g, :],
+                    out=codes[:, g, :].bitcast(FP8X4),
+                    scales=scales[:, g, :],
                     in_=grouped[:, g].rearrange("q m t -> q (m t)"),
                 )
             return codes, scales
 
         def theta_piece(piece):
-            grouped = work.tile([P, 2, 256, 4], BF16, name="th_grouped", align_bytes=64)
+            grouped = work.tile([P, 2, PIECE, 4], BF16, name="th_grouped", align_bytes=64)
             for g in range(2):
                 copy_out(
-                    "vs"[g],
+                    g + 1,
                     grouped[:, g].rearrange("p (c i) t -> p c t i", i=4),
                     th_sb[piece][:, 4 * g : 4 * g + 4, :].rearrange("p t (c i) -> p c t i", i=4),
                 )
@@ -173,44 +179,51 @@ def tile_akgcn_pa_kernel(tc, x, adj, lam_raw, theta, out):
                 in_=grouped[:].rearrange("p g c t -> p (g c t)"),
             )
 
-        def first_product(x_codes, x_scales, h_grouped, h, k, engine):
+        def first_product(x_codes, x_scales, h_grouped, half, k):
             bank = banks.tile([P, 4, P], F32, name="h_bank", tag="bank")
-            piece = 2 * h + k // 2
+            piece = 2 * half + k // 2
             cols = slice(P * (k % 2), P * (k % 2) + P)
             for j in range(4):
-                rows = slice(P * j, P * j + P)
+                nodes = slice(P * j, P * j + P)
                 for g in range(2):
                     nc.tensor.matmul_mx(
                         out=bank[:, j, :],
-                        lhsT=x_codes[:, g, rows].bitcast(FP8X4),
-                        lhsT_scale=x_scales[:, g, rows],
+                        lhsT=x_codes[:, g, nodes].bitcast(FP8X4),
+                        lhsT_scale=x_scales[:, g, nodes],
                         rhs=th_codes[:, piece, g, cols].bitcast(FP8X4),
                         rhs_scale=th_scales[:, piece, g, cols],
                         start=(g == 0),
                         stop=(g == 1),
                     )
-            copy_out(engine, h_grouped[:, P * k : P * k + P, :], bank[:].rearrange("p j c -> p c j"))
+            copy_out(0, h_grouped[:, P * k : P * k + P, :], bank[:].rearrange("p j c -> p c j"))
 
-        def second_product(u, h_codes, h_scales, i, engine):
-            bt, h = u // 2, u % 2
-            b = bt // T
+        def h_quantise(h_grouped):
+            codes = work.tile([P, HALF], U32, name="h_codes", align_bytes=64, bufs=4)
+            scales = work.tile([P, HALF], U8, name="h_scales", align_bytes=64, bufs=4)
+            nc.vector.quantize_mx(
+                out=codes[:].bitcast(FP8X4), scales=scales[:], in_=h_grouped[:].rearrange("p c j -> p (c j)")
+            )
+            return codes, scales
+
+        def second_product(unit, h_codes, h_scales, i):
+            s, half = divmod(unit, 2)
             rows = slice(P * i, P * i + P)
             bank = banks.tile([P, HALF], F32, name="o_bank", tag="bank")
             nc.tensor.matmul_mx(
                 out=bank[:],
-                lhsT=v_codes[b][:, rows].bitcast(FP8X4),
-                lhsT_scale=v_scales[b][:, rows],
+                lhsT=v_codes[s // T][:, rows].bitcast(FP8X4),
+                lhsT_scale=v_scales[s // T][:, rows],
                 rhs=h_codes[:].bitcast(FP8X4),
                 rhs_scale=h_scales[:],
                 start=True,
                 stop=True,
             )
             result = stage.tile([P, HALF], F32, name="result")
-            if engine == "s":
-                nc.scalar.activation(out=result[:], in_=bank[:], func=ACT.Relu)
+            if i % 2 == 0:
+                nc.scalar.activation(out=result[:], in_=bank[:], func=mybir.ActivationFunctionType.Relu)
             else:
                 nc.vector.tensor_scalar_max(out=result[:], in0=bank[:], scalar1=0.0)
-            nc.sync.dma_start(out=out[b, bt % T, rows, HALF * h : HALF * h + HALF], in_=result[:])
+            nc.sync.dma_start(out=out[s // T, s % T, rows, HALF * half : HALF * half + HALF], in_=result[:])
 
         v_sums(0)
         v_scale(0)
@@ -218,39 +231,34 @@ def tile_akgcn_pa_kernel(tc, x, adj, lam_raw, theta, out):
         theta_piece(0)
         theta_piece(1)
         v_quantise(0, v_transpose(0))
-        h_done = []
-        for n in range(4 * UNITS + LAG):
-            u, k = divmod(n, 4)
-            bt, h = divmod(u, 2)
-            if u < UNITS:
-                turn = h == 1 and bt + 1 < B * T
+        h_units = []
+        for n in range(BANKS + LAG):
+            unit, k = divmod(n, 4)
+            s, half = divmod(unit, 2)
+            if n < BANKS:
+                prepare_x = half == 1 and s + 1 < SLABS
                 if k == 0:
-                    if h == 0 and u > 0:
+                    if half == 0 and s > 0:
                         x_now = x_next
-                    if turn:
-                        x_grouped = x_transpose(bt + 1)
-                        if bt == T:
+                    if prepare_x:
+                        x_grouped = x_transpose(s + 1)
+                        if s == T:
                             v_grouped = v_transpose(1)
                     h_grouped = work.tile([P, HALF, 4], BF16, name="h_grouped", align_bytes=64)
-                    if u == 2:
+                    if unit == 2:
                         v_sums(1)
-                    if u == 3:
+                    if unit == 4:
                         v_scale(1)
-                if u == 0 and k % 2 == 0:
+                if unit == 0 and k % 2 == 0:
                     theta_piece(2 + k // 2)
-                first_product(x_now[0], x_now[1], h_grouped, h, k, (H_OUT_FIRST if bt == 0 else H_OUT)[k])
+                first_product(x_now[0], x_now[1], h_grouped, half, k)
             if n >= LAG:
-                w, i = divmod(n - LAG, 4)
-                second_product(w, h_done[w][0], h_done[w][1], i, O_OUT[i])
-            if u < UNITS:
-                if turn and k == 0:
+                old, i = divmod(n - LAG, 4)
+                second_product(old, h_units[old][0], h_units[old][1], i)
+            if n < BANKS:
+                if prepare_x and k == 0:
                     x_next = x_quantise(x_grouped)
-                if turn and k == 1 and bt == T:
+                if prepare_x and k == 1 and s == T:
                     v_quantise(1, v_grouped)
                 if k == 3:
-                    h_codes = work.tile([P, HALF], U32, name="h_codes", align_bytes=64, bufs=4)
-                    h_scales = work.tile([P, HALF], U8, name="h_scales", align_bytes=64, bufs=4)
-                    nc.vector.quantize_mx(
-                        out=h_codes[:].bitcast(FP8X4), scales=h_scales[:], in_=h_grouped[:].rearrange("p c j -> p (c j)")
-                    )
-                    h_done.append((h_codes, h_scales))
+                    h_units.append(h_quantise(h_grouped))

@@ -9,6 +9,7 @@ U32 = mybir.dt.uint32
 U8 = mybir.dt.uint8
 FP8X4 = mybir.dt.float8_e4m3fn_x4
 ALU = mybir.AluOpType
+ACT = mybir.ActivationFunctionType
 
 P = 128
 B, T, N, C = 2, 2, 512, 1024
@@ -82,32 +83,38 @@ def tile_akgcn_pa_kernel(tc, x, adj, lam_raw, theta, out):
         v_codes = [keep.tile([P, N], U32, name="v_codes%d" % b, align_bytes=64) for b in range(B)]
         v_scales = [keep.tile([P, N], U8, name="v_scales%d" % b, align_bytes=64) for b in range(B)]
         v_rows = [keep.tile([P, 4, N], BF16, name="v_rows%d" % b) for b in range(B)]
-        inverse = [keep.tile([P, 4], F32, name="inverse%d" % b) for b in range(B)]
+        inverse = [keep.tile([P, 16], F32, name="inverse%d" % b) for b in range(B)]
         with_diag = [keep.tile([P, 4, P], F32, name="with_diag%d" % b) for b in range(B)]
 
         def v_sums(b):
             rows = adj_sb[b][:, 0 : 4 * N].rearrange("p (i m) -> p i m", i=4)
-            nc.vector.tensor_reduce(out=inverse[b][:], in_=rows, axis=mybir.AxisListType.X, op=ALU.add)
-            nc.vector.tensor_scalar(out=inverse[b][:], in0=inverse[b][:], scalar1=r[:, 0:1], scalar2=None, op0=ALU.add)
-            nc.vector.reciprocal(out=inverse[b][:], in_=inverse[b][:])
+            for c in range(2):
+                unused = work.tile([P, N], BF16, name="unused")
+                nc.scalar.activation(
+                    out=unused[:], in_=rows[:, 2 + c, :], func=ACT.Copy, accum_out=inverse[b][:, 8 + c : 9 + c]
+                )
+            nc.vector.tensor_reduce(out=inverse[b][:, 0:2], in_=rows[:, 0:2, :], axis=mybir.AxisListType.X, op=ALU.add)
             nc.vector.tensor_tensor(
                 out=with_diag[b][:],
                 in0=adj_sb[b][:].rearrange("p (i s) -> p i s", s=N + P)[:, :, 0:P],
                 in1=r_eye[:].unsqueeze(1).to_broadcast([P, 4, P]),
                 op=ALU.add,
             )
+            sums = inverse[b][:].rearrange("p (a c) -> p a c", a=2)[:, :, 0:2]
+            nc.vector.tensor_scalar(out=sums, in0=sums, scalar1=r[:, 0:1], scalar2=None, op0=ALU.add)
+            nc.vector.reciprocal(out=sums, in_=sums)
 
         def v_scale(b):
             rows = adj_sb[b][:, 0 : 4 * N].rearrange("p (i m) -> p i m", i=4)
             for i in range(4):
                 nc.vector.tensor_scalar(
-                    out=v_rows[b][:, i, :], in0=rows[:, i, :], scalar1=inverse[b][:, i : i + 1], scalar2=None, op0=ALU.mult
+                    out=v_rows[b][:, i, :], in0=rows[:, i, :], scalar1=inverse[b][:, 8 * (i // 2) + i % 2 : 8 * (i // 2) + i % 2 + 1], scalar2=None, op0=ALU.mult
                 )
             for i in range(4):
                 nc.vector.tensor_scalar(
                     out=v_rows[b][:, i, P * i : P * i + P],
                     in0=with_diag[b][:, i, :],
-                    scalar1=inverse[b][:, i : i + 1],
+                    scalar1=inverse[b][:, 8 * (i // 2) + i % 2 : 8 * (i // 2) + i % 2 + 1],
                     scalar2=None,
                     op0=ALU.mult,
                 )
@@ -148,7 +155,7 @@ def tile_akgcn_pa_kernel(tc, x, adj, lam_raw, theta, out):
                                 identity=ident_f[:],
                             )
                     copy_out(
-                        g,
+                        g if s > 0 else 0,
                         grouped[:].bitcast(F32)[:, g, 256 * pair : 256 * pair + 256, :],
                         bank[:].rearrange("q u m -> q m u"),
                     )
@@ -220,7 +227,7 @@ def tile_akgcn_pa_kernel(tc, x, adj, lam_raw, theta, out):
             )
             result = stage.tile([P, HALF], F32, name="result")
             if i % 2 == 0:
-                nc.scalar.activation(out=result[:], in_=bank[:], func=mybir.ActivationFunctionType.Relu)
+                nc.scalar.activation(out=result[:], in_=bank[:], func=ACT.Relu)
             else:
                 nc.vector.tensor_scalar_max(out=result[:], in0=bank[:], scalar1=0.0)
             nc.sync.dma_start(out=out[s // T, s % T, rows, HALF * half : HALF * half + HALF], in_=result[:])
@@ -247,7 +254,7 @@ def tile_akgcn_pa_kernel(tc, x, adj, lam_raw, theta, out):
                     h_grouped = work.tile([P, HALF, 4], BF16, name="h_grouped", align_bytes=64)
                     if unit == 2:
                         v_sums(1)
-                    if unit == 4:
+                    if unit == 3:
                         v_scale(1)
                 if unit == 0 and k % 2 == 0:
                     theta_piece(2 + k // 2)

@@ -40,7 +40,7 @@ def tile_akgcn_pa_kernel(tc, x, adj, lam_raw, theta, out):
         lam_sb = keep.tile([P, 1], BF16, name="lam_sb")
         adj_sb = [keep.tile([P, 5 * N], BF16, name="adj%d" % b) for b in range(B)]
         x_sb = [keep.tile([P, 4, C], BF16, name="x%d" % s) for s in range(SLABS)]
-        th_sb = [keep.tile([P, 8, PIECE], BF16, name="th%d" % piece) for piece in range(4)]
+        th_sb = [keep.tile([P, 8, HALF], BF16, name="th%d" % half) for half in range(2)]
 
         def load_adj(b):
             nc.sync.dma_start(
@@ -53,17 +53,17 @@ def tile_akgcn_pa_kernel(tc, x, adj, lam_raw, theta, out):
             for pair in range(2):
                 nc.sync.dma_start(out=x_sb[s][:, 2 * pair : 2 * pair + 2, :], in_=rows[:, 2 * pair : 2 * pair + 2, :])
 
-        def load_theta(piece):
+        def load_theta(half):
             src = theta.rearrange("(t q e) c -> q t e c", t=4, q=P, e=2)
-            dst = th_sb[piece][:].rearrange("q (t e) c -> q t e c", e=2)
+            dst = th_sb[half][:].rearrange("q (t e) c -> q t e c", e=2)
             for e in range(2):
-                nc.sync.dma_start(out=dst[:, :, e, :], in_=src[:, :, e, PIECE * piece : PIECE * piece + PIECE])
+                nc.sync.dma_start(out=dst[:, :, e, :], in_=src[:, :, e, HALF * half : HALF * half + HALF])
 
         nc.scalar.dma_start(out=lam_sb[:], in_=lam_raw.partition_broadcast(P))
         load_adj(0)
         load_x(0)
-        for piece in range(4):
-            load_theta(piece)
+        for half in range(2):
+            load_theta(half)
         load_x(1)
         load_adj(1)
         load_x(2)
@@ -174,11 +174,12 @@ def tile_akgcn_pa_kernel(tc, x, adj, lam_raw, theta, out):
 
         def theta_piece(piece):
             grouped = work.tile([P, 2, PIECE, 4], BF16, name="th_grouped", align_bytes=64)
+            lo = PIECE * (piece % 2)
             for g in range(2):
                 copy_out(
                     g + 1,
                     grouped[:, g].rearrange("p (c i) t -> p c t i", i=4),
-                    th_sb[piece][:, 4 * g : 4 * g + 4, :].rearrange("p t (c i) -> p c t i", i=4),
+                    th_sb[piece // 2][:, 4 * g : 4 * g + 4, lo : lo + PIECE].rearrange("p t (c i) -> p c t i", i=4),
                 )
             nc.vector.quantize_mx(
                 out=th_codes[:, piece].rearrange("p g c -> p (g c)").bitcast(FP8X4),

@@ -49,9 +49,9 @@ def tile_akgcn_pa_kernel(tc, x, adj, lam_raw, theta, out):
             )
 
         def load_x(s):
-            rows = x[s // T, s % T].rearrange("(j p) c -> p j c", p=P)
-            for pair in range(2):
-                nc.sync.dma_start(out=x_sb[s][:, 2 * pair : 2 * pair + 2, :], in_=rows[:, 2 * pair : 2 * pair + 2, :])
+            rows = x[s // T, s % T].rearrange("(u p e) c -> p u e c", p=P, e=2)
+            for u in range(2):
+                nc.sync.dma_start(out=x_sb[s][:, 2 * u : 2 * u + 2, :], in_=rows[:, u])
 
         def load_theta(half):
             src = theta.rearrange("(t q e) c -> q t e c", t=4, q=P, e=2)
@@ -71,12 +71,8 @@ def tile_akgcn_pa_kernel(tc, x, adj, lam_raw, theta, out):
 
         ident_f = keep.tile([P, P], F32, name="ident_f")
         make_identity(nc, ident_f[:])
-        ident_b = keep.tile([P, P], BF16, name="ident_b")
-        make_identity(nc, ident_b[:])
         r = keep.tile([P, 1], F32, name="r")
-        nc.vector.tensor_scalar_max(out=r[:], in0=lam_sb[:], scalar1=0.0)
         r_eye = keep.tile([P, P], F32, name="r_eye")
-        nc.vector.tensor_scalar(out=r_eye[:], in0=ident_f[:], scalar1=r[:, 0:1], scalar2=None, op0=ALU.mult)
 
         th_codes = keep.tile([P, 4, 2, PIECE], U32, name="th_codes", align_bytes=64)
         th_scales = keep.tile([P, 4, 2, PIECE], U8, name="th_scales", align_bytes=64)
@@ -94,6 +90,12 @@ def tile_akgcn_pa_kernel(tc, x, adj, lam_raw, theta, out):
                     out=unused[:], in_=rows[:, 2 + c, :], func=ACT.Copy, accum_out=inverse[b][:, 8 + c : 9 + c]
                 )
             nc.vector.tensor_reduce(out=inverse[b][:, 0:2], in_=rows[:, 0:2, :], axis=mybir.AxisListType.X, op=ALU.add)
+
+        def r_on_diagonal():
+            nc.vector.tensor_scalar_max(out=r[:], in0=lam_sb[:], scalar1=0.0)
+            nc.vector.tensor_scalar(out=r_eye[:], in0=ident_f[:], scalar1=r[:, 0:1], scalar2=None, op0=ALU.mult)
+
+        def v_inverse(b):
             nc.vector.tensor_tensor(
                 out=with_diag[b][:],
                 in0=adj_sb[b][:].rearrange("p (i s) -> p i s", s=N + P)[:, :, 0:P],
@@ -120,18 +122,27 @@ def tile_akgcn_pa_kernel(tc, x, adj, lam_raw, theta, out):
                 )
 
         def v_transpose(b):
+            words = v_rows[b][:].bitcast(F32)
+            pairs = []
+            for pair in range(2):
+                bank = banks.tile([P, 2, 256], F32, name="v_bank", tag="bank")
+                for i in range(2):
+                    for u in range(2):
+                        nc.tensor.transpose(
+                            out=bank[:, u, P * i : P * i + P],
+                            in_=words[:, 2 * pair + i, P * u : P * u + P],
+                            identity=ident_f[:],
+                        )
+                pairs.append(bank)
+            return pairs
+
+        def v_copy_out(pairs, turns):
             grouped = work.tile([P, N, 4], BF16, name="v_grouped", align_bytes=64)
             for pair in range(2):
-                bank = banks.tile([P, 2, 4, P], BF16, name="v_bank", tag="bank")
-                for i in range(2):
-                    for j in range(4):
-                        nc.tensor.transpose(
-                            out=bank[:, i, j, :], in_=v_rows[b][:, 2 * pair + i, P * j : P * j + P], identity=ident_b[:]
-                        )
                 copy_out(
-                    pair,
-                    grouped[:, 256 * pair : 256 * pair + 256, :].rearrange("p (i n) j -> p i n j", i=2),
-                    bank[:].rearrange("p i j n -> p i n j"),
+                    turns[pair],
+                    grouped[:].bitcast(F32)[:, 256 * pair : 256 * pair + 256, :],
+                    pairs[pair][:].rearrange("p u n -> p n u"),
                 )
             return grouped
 
@@ -140,54 +151,51 @@ def tile_akgcn_pa_kernel(tc, x, adj, lam_raw, theta, out):
                 out=v_codes[b][:].bitcast(FP8X4), scales=v_scales[b][:], in_=grouped[:].rearrange("p n j -> p (n j)")
             )
 
-        def x_transpose(s):
+        def x_transpose(s, turns):
             words = x_sb[s][:].bitcast(F32)
             grouped = work.tile([P, 2, N, 4], BF16, name="x_grouped", align_bytes=64)
-            for pair in range(2):
+            codes = work.tile([P, 2, N], U32, name="x_codes", align_bytes=64, bufs=3)
+            scales = work.tile([P, 2, N], U8, name="x_scales", align_bytes=64, bufs=3)
+            for j in range(4):
+                bank = banks.tile([P, 2, 2, P], F32, name="x_bank", tag="bank")
                 for g in range(2):
-                    bank = banks.tile([P, 2, 256], F32, name="x_bank", tag="bank")
-                    for jj in range(2):
-                        for u in range(2):
-                            lo = 256 * g + P * u
-                            nc.tensor.transpose(
-                                out=bank[:, u, P * jj : P * jj + P],
-                                in_=words[:, 2 * pair + jj, lo : lo + P],
-                                identity=ident_f[:],
-                            )
-                    copy_out(
-                        g if s > 0 else 0,
-                        grouped[:].bitcast(F32)[:, g, 256 * pair : 256 * pair + 256, :],
-                        bank[:].rearrange("q u m -> q m u"),
-                    )
-            return grouped
-
-        def x_quantise(grouped):
-            codes = work.tile([P, 2, N], U32, name="x_codes", align_bytes=64)
-            scales = work.tile([P, 2, N], U8, name="x_scales", align_bytes=64)
-            for g in range(2):
-                nc.vector.quantize_mx(
-                    out=codes[:, g, :].bitcast(FP8X4),
-                    scales=scales[:, g, :],
-                    in_=grouped[:, g].rearrange("q m t -> q (m t)"),
+                    for u in range(2):
+                        lo = 256 * g + P * u
+                        nc.tensor.transpose(out=bank[:, g, u, :], in_=words[:, j, lo : lo + P], identity=ident_f[:])
+                copy_out(
+                    turns[j],
+                    grouped[:].bitcast(F32)[:, :, P * j : P * j + P, :],
+                    bank[:].rearrange("q g u p -> q g p u"),
                 )
-            return codes, scales
+            return grouped, codes, scales
 
-        def theta_piece(piece):
+        def x_quantise(xt, g, lo, hi):
+            grouped, codes, scales = xt
+            nc.vector.quantize_mx(
+                out=codes[:, g, lo:hi].bitcast(FP8X4),
+                scales=scales[:, g, lo:hi],
+                in_=grouped[:, g, lo:hi, :].rearrange("q m t -> q (m t)"),
+            )
+
+        def theta_copy(piece):
             grouped = work.tile([P, 2, PIECE, 4], BF16, name="th_grouped", align_bytes=64)
             lo = PIECE * (piece % 2)
-            for g in range(2):
+            for g in (1, 0):
                 copy_out(
-                    g + 1,
+                    1 - g,
                     grouped[:, g].rearrange("p (c i) t -> p c t i", i=4),
                     th_sb[piece // 2][:, 4 * g : 4 * g + 4, lo : lo + PIECE].rearrange("p t (c i) -> p c t i", i=4),
                 )
+            return grouped
+
+        def theta_quantise(piece, grouped):
             nc.vector.quantize_mx(
                 out=th_codes[:, piece].rearrange("p g c -> p (g c)").bitcast(FP8X4),
                 scales=th_scales[:, piece].rearrange("p g c -> p (g c)"),
                 in_=grouped[:].rearrange("p g c t -> p (g c t)"),
             )
 
-        def first_product(x_codes, x_scales, h_grouped, half, k):
+        def first_product(xt, h, half, k):
             bank = banks.tile([P, 4, P], F32, name="h_bank", tag="bank")
             piece = 2 * half + k // 2
             cols = slice(P * (k % 2), P * (k % 2) + P)
@@ -196,24 +204,30 @@ def tile_akgcn_pa_kernel(tc, x, adj, lam_raw, theta, out):
                 for g in range(2):
                     nc.tensor.matmul_mx(
                         out=bank[:, j, :],
-                        lhsT=x_codes[:, g, nodes].bitcast(FP8X4),
-                        lhsT_scale=x_scales[:, g, nodes],
+                        lhsT=xt[1][:, g, nodes].bitcast(FP8X4),
+                        lhsT_scale=xt[2][:, g, nodes],
                         rhs=th_codes[:, piece, g, cols].bitcast(FP8X4),
                         rhs_scale=th_scales[:, piece, g, cols],
                         start=(g == 0),
                         stop=(g == 1),
                     )
-            copy_out(0, h_grouped[:, P * k : P * k + P, :], bank[:].rearrange("p j c -> p c j"))
+            copy_out(0, h[0][:, P * k : P * k + P, :], bank[:].rearrange("p j c -> p c j"))
 
-        def h_quantise(h_grouped):
-            codes = work.tile([P, HALF], U32, name="h_codes", align_bytes=64, bufs=4)
-            scales = work.tile([P, HALF], U8, name="h_scales", align_bytes=64, bufs=4)
+        def h_tiles():
+            grouped = work.tile([P, HALF, 4], BF16, name="h_grouped", align_bytes=64, bufs=3)
+            codes = work.tile([P, HALF], U32, name="h_codes", align_bytes=64, bufs=5)
+            scales = work.tile([P, HALF], U8, name="h_scales", align_bytes=64, bufs=5)
+            return grouped, codes, scales
+
+        def h_quantise(h, lo, hi):
+            grouped, codes, scales = h
             nc.vector.quantize_mx(
-                out=codes[:].bitcast(FP8X4), scales=scales[:], in_=h_grouped[:].rearrange("p c j -> p (c j)")
+                out=codes[:, lo:hi].bitcast(FP8X4),
+                scales=scales[:, lo:hi],
+                in_=grouped[:, lo:hi, :].rearrange("p c j -> p (c j)"),
             )
-            return codes, scales
 
-        def second_product(unit, h_codes, h_scales, i):
+        def second_product(unit, h, i):
             s, half = divmod(unit, 2)
             rows = slice(P * i, P * i + P)
             bank = banks.tile([P, HALF], F32, name="o_bank", tag="bank")
@@ -221,8 +235,8 @@ def tile_akgcn_pa_kernel(tc, x, adj, lam_raw, theta, out):
                 out=bank[:],
                 lhsT=v_codes[s // T][:, rows].bitcast(FP8X4),
                 lhsT_scale=v_scales[s // T][:, rows],
-                rhs=h_codes[:].bitcast(FP8X4),
-                rhs_scale=h_scales[:],
+                rhs=h[1][:].bitcast(FP8X4),
+                rhs_scale=h[2][:],
                 start=True,
                 stop=True,
             )
@@ -233,40 +247,87 @@ def tile_akgcn_pa_kernel(tc, x, adj, lam_raw, theta, out):
                 nc.vector.tensor_scalar_max(out=result[:], in0=bank[:], scalar1=0.0)
             nc.sync.dma_start(out=out[s // T, s % T, rows, HALF * half : HALF * half + HALF], in_=result[:])
 
+        def second_product_quarter(unit, h, quarter, pair):
+            s, half = divmod(unit, 2)
+            cols = slice(PIECE * quarter, PIECE * quarter + PIECE)
+            bank = banks.tile([P, 2, PIECE], F32, name="q_bank", tag="bank")
+            for i in range(2):
+                rows = slice(P * (2 * pair + i), P * (2 * pair + i) + P)
+                nc.tensor.matmul_mx(
+                    out=bank[:, i, :],
+                    lhsT=v_codes[s // T][:, rows].bitcast(FP8X4),
+                    lhsT_scale=v_scales[s // T][:, rows],
+                    rhs=h[1][:, cols].bitcast(FP8X4),
+                    rhs_scale=h[2][:, cols],
+                    start=True,
+                    stop=True,
+                )
+            result = stage.tile([P, 2, PIECE], F32, name="q_result")
+            if pair == 0:
+                nc.scalar.activation(out=result[:], in_=bank[:], func=ACT.Relu)
+            else:
+                nc.vector.tensor_scalar_max(out=result[:], in0=bank[:], scalar1=0.0)
+            lo = HALF * half + PIECE * quarter
+            rows = out[s // T, s % T, 256 * pair : 256 * pair + 256, lo : lo + PIECE]
+            nc.sync.dma_start(out=rows.rearrange("(i p) c -> p i c", p=P), in_=result[:])
+
         v_sums(0)
+        r_on_diagonal()
+        v_inverse(0)
         v_scale(0)
-        x_now = x_quantise(x_transpose(0))
-        theta_piece(0)
-        theta_piece(1)
-        v_quantise(0, v_transpose(0))
-        h_units = []
-        for n in range(BANKS + LAG):
+        xt = x_transpose(0, (0, 0, 0, 0))
+        v_pairs = v_transpose(0)
+        for g in range(2):
+            x_quantise(xt, g, 0, 256)
+        th_grouped = theta_copy(0)
+        for g in range(2):
+            x_quantise(xt, g, 256, 512)
+        theta_quantise(0, th_grouped)
+        for piece in range(1, 4):
+            th_grouped = theta_copy(piece)
+            theta_quantise(piece, th_grouped)
+        slabs = [xt]
+        units = []
+        done = 0
+        for n in range(BANKS):
             unit, k = divmod(n, 4)
             s, half = divmod(unit, 2)
-            if n < BANKS:
-                prepare_x = half == 1 and s + 1 < SLABS
-                if k == 0:
-                    if half == 0 and s > 0:
-                        x_now = x_next
-                    if prepare_x:
-                        x_grouped = x_transpose(s + 1)
-                        if s == T:
-                            v_grouped = v_transpose(1)
-                    h_grouped = work.tile([P, HALF, 4], BF16, name="h_grouped", align_bytes=64)
-                    if unit == 2:
-                        v_sums(1)
-                    if unit == 3:
-                        v_scale(1)
-                if unit == 0 and k % 2 == 0:
-                    theta_piece(2 + k // 2)
-                first_product(x_now[0], x_now[1], h_grouped, half, k)
-            if n >= LAG:
-                old, i = divmod(n - LAG, 4)
-                second_product(old, h_units[old][0], h_units[old][1], i)
-            if n < BANKS:
-                if prepare_x and k == 0:
-                    x_next = x_quantise(x_grouped)
-                if prepare_x and k == 1 and s == T:
-                    v_quantise(1, v_grouped)
-                if k == 3:
-                    h_units.append(h_quantise(h_grouped))
+            if n in (2, 8, 14):
+                xt = x_transpose(len(slabs), (0, 1, 0, 1))
+                slabs.append(xt)
+            if n == 18:
+                v_pairs = v_transpose(1)
+            if k == 0:
+                h = h_tiles()
+                units.append(h)
+            first_product(slabs[s], units[unit], half, k)
+            if k == 0 and unit > 0:
+                h_quantise(units[unit - 1], 0, HALF)
+            while done < n - 8 + max(0, (n - 20) // 2):
+                second_product(done // 4, units[done // 4], done % 4)
+                done += 1
+            if n in (3, 9, 15):
+                x_quantise(slabs[-1], 0, 0, N)
+            if n in (4, 10, 16):
+                x_quantise(slabs[-1], 1, 0, N)
+            if n == 4:
+                v_grouped = v_copy_out(v_pairs, (1, 0))
+            if n == 6:
+                v_quantise(0, v_grouped)
+            if n == 10:
+                v_sums(1)
+                v_inverse(1)
+            if n == 14:
+                v_scale(1)
+            if n == 30:
+                h_quantise(units[7], 0, PIECE)
+            if n == 18:
+                v_grouped = v_copy_out(v_pairs, (1, 1))
+                v_quantise(1, v_grouped)
+        while done < 28:
+            second_product(done // 4, units[done // 4], done % 4)
+            done += 1
+        h_quantise(units[7], PIECE, HALF)
+        for quarter in range(2):
+            for pair in range(2):
+                second_product_quarter(7, units[7], quarter, pair)

@@ -178,7 +178,7 @@ def tile_akgcn_pa_kernel(tc, x, adj, lam_raw, theta, out):
             )
 
         def theta_copy(piece):
-            grouped = work.tile([P, 2, PIECE, 4], BF16, name="th_grouped", align_bytes=64)
+            grouped = work.tile([P, 2, PIECE, 4], BF16, name="th_grouped", align_bytes=64, bufs=3)
             lo = PIECE * (piece % 2)
             for g in (1, 0):
                 copy_out(
@@ -247,10 +247,10 @@ def tile_akgcn_pa_kernel(tc, x, adj, lam_raw, theta, out):
                 nc.vector.tensor_scalar_max(out=result[:], in0=bank[:], scalar1=0.0)
             nc.sync.dma_start(out=out[s // T, s % T, rows, HALF * half : HALF * half + HALF], in_=result[:])
 
-        def second_product_quarter(unit, h, quarter, pair):
+        def second_product_part(unit, h, start, width, pair):
             s, half = divmod(unit, 2)
-            cols = slice(PIECE * quarter, PIECE * quarter + PIECE)
-            bank = banks.tile([P, 2, PIECE], F32, name="q_bank", tag="bank")
+            cols = slice(start, start + width)
+            bank = banks.tile([P, 2, width], F32, name="part_bank", tag="bank")
             for i in range(2):
                 rows = slice(P * (2 * pair + i), P * (2 * pair + i) + P)
                 nc.tensor.matmul_mx(
@@ -262,13 +262,13 @@ def tile_akgcn_pa_kernel(tc, x, adj, lam_raw, theta, out):
                     start=True,
                     stop=True,
                 )
-            result = stage.tile([P, 2, PIECE], F32, name="q_result")
+            result = stage.tile([P, 2, width], F32, name="part_result", bufs=6)
             if pair == 0:
                 nc.scalar.activation(out=result[:], in_=bank[:], func=ACT.Relu)
             else:
                 nc.vector.tensor_scalar_max(out=result[:], in0=bank[:], scalar1=0.0)
-            lo = HALF * half + PIECE * quarter
-            rows = out[s // T, s % T, 256 * pair : 256 * pair + 256, lo : lo + PIECE]
+            lo = HALF * half + start
+            rows = out[s // T, s % T, 256 * pair : 256 * pair + 256, lo : lo + width]
             nc.sync.dma_start(out=rows.rearrange("(i p) c -> p i c", p=P), in_=result[:])
 
         v_sums(0)
@@ -283,9 +283,13 @@ def tile_akgcn_pa_kernel(tc, x, adj, lam_raw, theta, out):
         for g in range(2):
             x_quantise(xt, g, 256, 512)
         theta_quantise(0, th_grouped)
+        pieces = [th_grouped]
         for piece in range(1, 4):
             th_grouped = theta_copy(piece)
-            theta_quantise(piece, th_grouped)
+            pieces.append(th_grouped)
+            if piece > 1:
+                theta_quantise(piece - 1, pieces[piece - 1])
+        theta_quantise(3, pieces[3])
         slabs = [xt]
         units = []
         done = 0
@@ -320,14 +324,16 @@ def tile_akgcn_pa_kernel(tc, x, adj, lam_raw, theta, out):
             if n == 14:
                 v_scale(1)
             if n == 30:
-                h_quantise(units[7], 0, PIECE)
+                h_quantise(units[7], 0, 256)
+            if n == 31:
+                h_quantise(units[7], 256, 384)
             if n == 18:
                 v_grouped = v_copy_out(v_pairs, (1, 1))
                 v_quantise(1, v_grouped)
         while done < 28:
             second_product(done // 4, units[done // 4], done % 4)
             done += 1
-        h_quantise(units[7], PIECE, HALF)
-        for quarter in range(2):
+        h_quantise(units[7], 384, 512)
+        for start, width in ((0, 256), (256, 128), (384, 128)):
             for pair in range(2):
-                second_product_quarter(7, units[7], quarter, pair)
+                second_product_part(7, units[7], start, width, pair)

from contextlib import ExitStack

import concourse.mybir as mybir
from concourse.masks import make_identity

F32 = mybir.dt.float32
BF16 = mybir.dt.bfloat16
U32 = mybir.dt.uint32
U8 = mybir.dt.uint8
FP8X4 = mybir.dt.float8_e4m3fn_x4
ALU = mybir.AluOpType
ACT = mybir.ActivationFunctionType

P = 128
B, T, N, C = 2, 2, 512, 1024
FLOPS = 2 * B * T * N * C * C + 2 * B * T * N * N * C

SLABS = B * T
HALF = C // 2
PIECE = C // 4
BANKS = 8 * SLABS
LAG = 8


def tile_akgcn_pa_kernel(tc, x, adj, lam_raw, theta, out):
    nc = tc.nc
    with ExitStack() as ctx:
        keep = ctx.enter_context(tc.tile_pool(name="keep", bufs=1))
        work = ctx.enter_context(tc.tile_pool(name="work", bufs=2))
        stage = ctx.enter_context(tc.tile_pool(name="stage", bufs=12))
        banks = ctx.enter_context(tc.psum_pool(name="banks", bufs=8))
        ctx.enter_context(tc.manual_schedule())

        def copy_out(turn, dst, src):
            if turn % 2 == 0:
                nc.scalar.copy(out=dst, in_=src)
            else:
                nc.vector.tensor_copy(out=dst, in_=src)

        lam_sb = keep.tile([P, 1], BF16, name="lam_sb")
        adj_sb = [keep.tile([P, 5 * N], BF16, name="adj%d" % b) for b in range(B)]
        x_sb = [keep.tile([P, 4, C], BF16, name="x%d" % s) for s in range(SLABS)]
        th_sb = [keep.tile([P, 8, HALF], BF16, name="th%d" % half) for half in range(2)]

        def load_adj(b):
            nc.sync.dma_start(
                out=adj_sb[b][:, 0 : 4 * N].rearrange("p (i m) -> p i m", i=4),
                in_=adj[b].rearrange("(i p) m -> p i m", p=P),
            )

        def load_x(s):
            rows = x[s // T, s % T].rearrange("(u p e) c -> p u e c", p=P, e=2)
            for u in range(2):
                nc.sync.dma_start(out=x_sb[s][:, 2 * u : 2 * u + 2, :], in_=rows[:, u])

        def load_theta(half):
            src = theta.rearrange("(t q e) c -> q t e c", t=4, q=P, e=2)
            dst = th_sb[half][:].rearrange("q (t e) c -> q t e c", e=2)
            for e in range(2):
                nc.sync.dma_start(out=dst[:, :, e, :], in_=src[:, :, e, HALF * half : HALF * half + HALF])

        nc.scalar.dma_start(out=lam_sb[:], in_=lam_raw.partition_broadcast(P))
        load_adj(0)
        load_x(0)
        for half in range(2):
            load_theta(half)
        load_x(1)
        load_adj(1)
        load_x(2)
        load_x(3)

        ident_f = keep.tile([P, P], F32, name="ident_f")
        make_identity(nc, ident_f[:])
        r = keep.tile([P, 1], F32, name="r")
        r_eye = keep.tile([P, P], F32, name="r_eye")

        th_codes = keep.tile([P, 4, 2, PIECE], U32, name="th_codes", align_bytes=64)
        th_scales = keep.tile([P, 4, 2, PIECE], U8, name="th_scales", align_bytes=64)
        v_codes = [keep.tile([P, N], U32, name="v_codes%d" % b, align_bytes=64) for b in range(B)]
        v_scales = [keep.tile([P, N], U8, name="v_scales%d" % b, align_bytes=64) for b in range(B)]
        v_rows = [keep.tile([P, 4, N], BF16, name="v_rows%d" % b) for b in range(B)]
        inverse = [keep.tile([P, 16], F32, name="inverse%d" % b) for b in range(B)]
        with_diag = [keep.tile([P, 4, P], F32, name="with_diag%d" % b) for b in range(B)]

        def v_sums(b):
            rows = adj_sb[b][:, 0 : 4 * N].rearrange("p (i m) -> p i m", i=4)
            for c in range(2):
                unused = work.tile([P, N], BF16, name="unused")
                nc.scalar.activation(
                    out=unused[:], in_=rows[:, 2 + c, :], func=ACT.Copy, accum_out=inverse[b][:, 8 + c : 9 + c]
                )
            nc.vector.tensor_reduce(out=inverse[b][:, 0:2], in_=rows[:, 0:2, :], axis=mybir.AxisListType.X, op=ALU.add)

        def r_on_diagonal():
            nc.vector.tensor_scalar_max(out=r[:], in0=lam_sb[:], scalar1=0.0)
            nc.vector.tensor_scalar(out=r_eye[:], in0=ident_f[:], scalar1=r[:, 0:1], scalar2=None, op0=ALU.mult)

        def v_inverse(b):
            nc.vector.tensor_tensor(
                out=with_diag[b][:],
                in0=adj_sb[b][:].rearrange("p (i s) -> p i s", s=N + P)[:, :, 0:P],
                in1=r_eye[:].unsqueeze(1).to_broadcast([P, 4, P]),
                op=ALU.add,
            )
            sums = inverse[b][:].rearrange("p (a c) -> p a c", a=2)[:, :, 0:2]
            nc.vector.tensor_scalar(out=sums, in0=sums, scalar1=r[:, 0:1], scalar2=None, op0=ALU.add)
            nc.vector.reciprocal(out=sums, in_=sums)

        def v_scale(b):
            rows = adj_sb[b][:, 0 : 4 * N].rearrange("p (i m) -> p i m", i=4)
            for i in range(4):
                nc.vector.tensor_scalar(
                    out=v_rows[b][:, i, :], in0=rows[:, i, :], scalar1=inverse[b][:, 8 * (i // 2) + i % 2 : 8 * (i // 2) + i % 2 + 1], scalar2=None, op0=ALU.mult
                )
            for i in range(4):
                nc.vector.tensor_scalar(
                    out=v_rows[b][:, i, P * i : P * i + P],
                    in0=with_diag[b][:, i, :],
                    scalar1=inverse[b][:, 8 * (i // 2) + i % 2 : 8 * (i // 2) + i % 2 + 1],
                    scalar2=None,
                    op0=ALU.mult,
                )

        def v_transpose(b):
            words = v_rows[b][:].bitcast(F32)
            pairs = []
            for pair in range(2):
                bank = banks.tile([P, 2, 256], F32, name="v_bank", tag="bank")
                for i in range(2):
                    for u in range(2):
                        nc.tensor.transpose(
                            out=bank[:, u, P * i : P * i + P],
                            in_=words[:, 2 * pair + i, P * u : P * u + P],
                            identity=ident_f[:],
                        )
                pairs.append(bank)
            return pairs

        def v_copy_out(pairs, turns):
            grouped = work.tile([P, N, 4], BF16, name="v_grouped", align_bytes=64)
            for pair in range(2):
                copy_out(
                    turns[pair],
                    grouped[:].bitcast(F32)[:, 256 * pair : 256 * pair + 256, :],
                    pairs[pair][:].rearrange("p u n -> p n u"),
                )
            return grouped

        def v_quantise(b, grouped):
            nc.vector.quantize_mx(
                out=v_codes[b][:].bitcast(FP8X4), scales=v_scales[b][:], in_=grouped[:].rearrange("p n j -> p (n j)")
            )

        def x_transpose(s, turns):
            words = x_sb[s][:].bitcast(F32)
            grouped = work.tile([P, 2, N, 4], BF16, name="x_grouped", align_bytes=64)
            codes = work.tile([P, 2, N], U32, name="x_codes", align_bytes=64, bufs=3)
            scales = work.tile([P, 2, N], U8, name="x_scales", align_bytes=64, bufs=3)
            for j in range(4):
                bank = banks.tile([P, 2, 2, P], F32, name="x_bank", tag="bank")
                for g in range(2):
                    for u in range(2):
                        lo = 256 * g + P * u
                        nc.tensor.transpose(out=bank[:, g, u, :], in_=words[:, j, lo : lo + P], identity=ident_f[:])
                copy_out(
                    turns[j],
                    grouped[:].bitcast(F32)[:, :, P * j : P * j + P, :],
                    bank[:].rearrange("q g u p -> q g p u"),
                )
            return grouped, codes, scales

        def x_quantise(xt, g, lo, hi):
            grouped, codes, scales = xt
            nc.vector.quantize_mx(
                out=codes[:, g, lo:hi].bitcast(FP8X4),
                scales=scales[:, g, lo:hi],
                in_=grouped[:, g, lo:hi, :].rearrange("q m t -> q (m t)"),
            )

        def theta_copy(piece):
            grouped = work.tile([P, 2, PIECE, 4], BF16, name="th_grouped", align_bytes=64, bufs=3)
            lo = PIECE * (piece % 2)
            for g in (1, 0):
                copy_out(
                    1 - g,
                    grouped[:, g].rearrange("p (c i) t -> p c t i", i=4),
                    th_sb[piece // 2][:, 4 * g : 4 * g + 4, lo : lo + PIECE].rearrange("p t (c i) -> p c t i", i=4),
                )
            return grouped

        def theta_quantise(piece, grouped):
            nc.vector.quantize_mx(
                out=th_codes[:, piece].rearrange("p g c -> p (g c)").bitcast(FP8X4),
                scales=th_scales[:, piece].rearrange("p g c -> p (g c)"),
                in_=grouped[:].rearrange("p g c t -> p (g c t)"),
            )

        def first_product(xt, h, half, k):
            bank = banks.tile([P, 4, P], F32, name="h_bank", tag="bank")
            piece = 2 * half + k // 2
            cols = slice(P * (k % 2), P * (k % 2) + P)
            for j in range(4):
                nodes = slice(P * j, P * j + P)
                for g in range(2):
                    nc.tensor.matmul_mx(
                        out=bank[:, j, :],
                        lhsT=xt[1][:, g, nodes].bitcast(FP8X4),
                        lhsT_scale=xt[2][:, g, nodes],
                        rhs=th_codes[:, piece, g, cols].bitcast(FP8X4),
                        rhs_scale=th_scales[:, piece, g, cols],
                        start=(g == 0),
                        stop=(g == 1),
                    )
            copy_out(0, h[0][:, P * k : P * k + P, :], bank[:].rearrange("p j c -> p c j"))

        def h_tiles():
            grouped = work.tile([P, HALF, 4], BF16, name="h_grouped", align_bytes=64, bufs=3)
            codes = work.tile([P, HALF], U32, name="h_codes", align_bytes=64, bufs=5)
            scales = work.tile([P, HALF], U8, name="h_scales", align_bytes=64, bufs=5)
            return grouped, codes, scales

        def h_quantise(h, lo, hi):
            grouped, codes, scales = h
            nc.vector.quantize_mx(
                out=codes[:, lo:hi].bitcast(FP8X4),
                scales=scales[:, lo:hi],
                in_=grouped[:, lo:hi, :].rearrange("p c j -> p (c j)"),
            )

        def second_product(unit, h, i):
            s, half = divmod(unit, 2)
            rows = slice(P * i, P * i + P)
            bank = banks.tile([P, HALF], F32, name="o_bank", tag="bank")
            nc.tensor.matmul_mx(
                out=bank[:],
                lhsT=v_codes[s // T][:, rows].bitcast(FP8X4),
                lhsT_scale=v_scales[s // T][:, rows],
                rhs=h[1][:].bitcast(FP8X4),
                rhs_scale=h[2][:],
                start=True,
                stop=True,
            )
            result = stage.tile([P, HALF], F32, name="result")
            if i % 2 == 0:
                nc.scalar.activation(out=result[:], in_=bank[:], func=ACT.Relu)
            else:
                nc.vector.tensor_scalar_max(out=result[:], in0=bank[:], scalar1=0.0)
            nc.sync.dma_start(out=out[s // T, s % T, rows, HALF * half : HALF * half + HALF], in_=result[:])

        def second_product_part(unit, h, start, width, pair):
            s, half = divmod(unit, 2)
            cols = slice(start, start + width)
            bank = banks.tile([P, 2, width], F32, name="part_bank", tag="bank")
            for i in range(2):
                rows = slice(P * (2 * pair + i), P * (2 * pair + i) + P)
                nc.tensor.matmul_mx(
                    out=bank[:, i, :],
                    lhsT=v_codes[s // T][:, rows].bitcast(FP8X4),
                    lhsT_scale=v_scales[s // T][:, rows],
                    rhs=h[1][:, cols].bitcast(FP8X4),
                    rhs_scale=h[2][:, cols],
                    start=True,
                    stop=True,
                )
            result = stage.tile([P, 2, width], F32, name="part_result", bufs=6)
            if pair == 0:
                nc.scalar.activation(out=result[:], in_=bank[:], func=ACT.Relu)
            else:
                nc.vector.tensor_scalar_max(out=result[:], in0=bank[:], scalar1=0.0)
            lo = HALF * half + start
            rows = out[s // T, s % T, 256 * pair : 256 * pair + 256, lo : lo + width]
            nc.sync.dma_start(out=rows.rearrange("(i p) c -> p i c", p=P), in_=result[:])

        v_sums(0)
        r_on_diagonal()
        v_inverse(0)
        v_scale(0)
        xt = x_transpose(0, (0, 0, 0, 0))
        v_pairs = v_transpose(0)
        for g in range(2):
            x_quantise(xt, g, 0, 256)
        th_grouped = theta_copy(0)
        for g in range(2):
            x_quantise(xt, g, 256, 512)
        theta_quantise(0, th_grouped)
        pieces = [th_grouped]
        for piece in range(1, 4):
            th_grouped = theta_copy(piece)
            pieces.append(th_grouped)
            if piece > 1:
                theta_quantise(piece - 1, pieces[piece - 1])
        theta_quantise(3, pieces[3])
        slabs = [xt]
        units = []
        done = 0
        for n in range(BANKS):
            unit, k = divmod(n, 4)
            s, half = divmod(unit, 2)
            if n in (2, 8, 14):
                xt = x_transpose(len(slabs), (0, 1, 0, 1))
                slabs.append(xt)
            if n == 18:
                v_pairs = v_transpose(1)
            if k == 0:
                h = h_tiles()
                units.append(h)
            first_product(slabs[s], units[unit], half, k)
            if k == 0 and unit > 0:
                h_quantise(units[unit - 1], 0, HALF)
            while done < n - 8 + max(0, (n - 20) // 2):
                second_product(done // 4, units[done // 4], done % 4)
                done += 1
            if n in (3, 9, 15):
                x_quantise(slabs[-1], 0, 0, N)
            if n in (4, 10, 16):
                x_quantise(slabs[-1], 1, 0, N)
            if n == 4:
                v_grouped = v_copy_out(v_pairs, (1, 0))
            if n == 6:
                v_quantise(0, v_grouped)
            if n == 10:
                v_sums(1)
                v_inverse(1)
            if n == 14:
                v_scale(1)
            if n == 30:
                h_quantise(units[7], 0, 256)
            if n == 31:
                h_quantise(units[7], 256, 384)
            if n == 18:
                v_grouped = v_copy_out(v_pairs, (1, 1))
                v_quantise(1, v_grouped)
        while done < 28:
            second_product(done // 4, units[done // 4], done % 4)
            done += 1
        h_quantise(units[7], 384, 512)
        for start, width in ((0, 256), (256, 128), (384, 128)):
            for pair in range(2):
                second_product_part(7, units[7], start, width, pair)
